import numpy as np
import ml_dtypes


def mxq(x, axis, fmt="e4m3"):
    dtype, down = {"e4m3": (ml_dtypes.float8_e4m3fn, 7), "e5m2": (ml_dtypes.float8_e5m2, 14)}[fmt]
    v = np.moveaxis(np.asarray(x, np.float32).astype(ml_dtypes.bfloat16).astype(np.float64), axis, -1)
    blocks = v.reshape(v.shape[:-1] + (-1, 32))
    amax = np.abs(blocks).max(-1, keepdims=True)
    byte = np.maximum(np.where(amax > 0, np.frexp(amax)[1] - 1 + 127, 0) - down, 1)
    scale = np.exp2(byte - 127.0)
    codes = (blocks / scale).astype(np.float32).astype(dtype).astype(np.float64)
    return np.moveaxis((codes * scale).reshape(v.shape), -1, axis)


WIDE = False


def mx_kscale(k):
    if not WIDE:
        return np.ones(k)
    levels = np.array([10, -10, 5, -5, 0])
    a = np.random.permutation(np.resize(levels, k // 512 * 4)).reshape(k // 512, 4)
    idx = np.arange(k)
    return np.exp2(a[idx // 512, idx % 128 // 32])


BF16 = ml_dtypes.bfloat16


def bf(x):
    return np.asarray(x, np.float32).astype(BF16)


def f64(x):
    return np.asarray(x).astype(np.float64)


E2M1 = np.array([0.0, 0.5, 1.0, 1.5, 2.0, 3.0, 4.0, 6.0, -0.0, -0.5, -1.0, -1.5, -2.0, -3.0, -4.0, -6.0])


def pack_weight(w, fmt):
    k, n = w.shape
    w = f64(bf(w)).reshape(k // 32, 32, n)
    amax = np.abs(w).max(1)
    if fmt == "e4m3":
        byte = np.frexp(amax)[1] - 1 + 127 - 7
    else:
        mant, ex = np.frexp(amax / 6.0)
        byte = np.where(mant > 0.5, ex, ex - 1) + 127
    byte = np.clip(np.where(amax > 0, byte, 1), 1, 254)
    scaled = (w * np.exp2(127.0 - byte)[:, None, :]).reshape(k, n).astype(np.float32)
    by_word = np.ascontiguousarray(scaled.reshape(k // 512, 128, 4, n).transpose(0, 1, 3, 2))
    if fmt == "e4m3":
        words = by_word.astype(ml_dtypes.float8_e4m3fn).view(np.uint8)
    else:
        c = by_word.astype(ml_dtypes.float4_e2m1fn).view(np.uint8) & 0xF
        words = c[..., 0::2] | (c[..., 1::2] << 4)
    return np.ascontiguousarray(words), np.ascontiguousarray(byte.astype(np.uint8).reshape(k // 512, 16, n))


def unpack_weight(words, scales, fmt):
    g, p, n, _ = words.shape
    if fmt == "e4m3":
        vals = np.ascontiguousarray(words).view(ml_dtypes.float8_e4m3fn).astype(np.float64)
    else:
        nib = np.empty((g, p, n, 4), np.uint8)
        nib[..., 0::2] = words & 0xF
        nib[..., 1::2] = words >> 4
        vals = E2M1[nib]
    vals = vals * np.repeat(np.exp2(scales.astype(np.float64) - 127.0), 8, axis=1)[..., None]
    return vals.transpose(0, 1, 3, 2).reshape(g * 512, n)


B, IN_DIM, R_IN, R_OUT = 4096, 1024, 512, 512
HIDDEN = R_IN + R_OUT
BASELINE_THRE = 0.1
BETA = 1.8
R_M = 3.0
DT = 1.0
FMT = "e4m3"


def sigmoid(v):
    return 1.0 / (1.0 + np.exp(-v))


def setup_inputs():
    s = mx_kscale(IN_DIM)
    x_t = bf(np.random.standard_normal((B, IN_DIM)) * s)
    spk_t = bf(np.random.random((B, HIDDEN)) < 0.3)
    mem_t_in = bf(np.random.standard_normal((B, R_IN)))
    b_t_in = bf(np.random.random((B, R_IN)))
    W_x2in = np.random.standard_normal((R_IN, IN_DIM)) / np.sqrt(IN_DIM) / s[None, :]
    b_x2in = bf(np.random.standard_normal(R_IN) * 0.5)
    W_rec4in = np.random.standard_normal((R_IN, R_IN)) * 1.5 / np.sqrt(R_IN)
    b_rec4in = bf(np.random.standard_normal(R_IN) * 0.5)
    W_out2in = np.random.standard_normal((R_IN, R_OUT)) * 1.5 / np.sqrt(R_OUT)
    b_out2in = bf(np.random.standard_normal(R_IN) * 0.5)
    tau_adp_in = bf(1.5 + 0.5 * np.random.standard_normal(R_IN))
    tau_m_in = bf(2.0 + 0.5 * np.random.standard_normal(R_IN))
    W_x2in_words, W_x2in_scales = pack_weight(np.ascontiguousarray(W_x2in.T), FMT)
    W_rec4in_words, W_rec4in_scales = pack_weight(np.ascontiguousarray(W_rec4in.T), FMT)
    W_out2in_words, W_out2in_scales = pack_weight(np.ascontiguousarray(W_out2in.T), FMT)
    return {
        "x_t": x_t,
        "spk_t": spk_t,
        "mem_t_in": mem_t_in,
        "b_t_in": b_t_in,
        "W_x2in_words": W_x2in_words,
        "W_x2in_scales": W_x2in_scales,
        "b_x2in": b_x2in,
        "W_rec4in_words": W_rec4in_words,
        "W_rec4in_scales": W_rec4in_scales,
        "b_rec4in": b_rec4in,
        "W_out2in_words": W_out2in_words,
        "W_out2in_scales": W_out2in_scales,
        "b_out2in": b_out2in,
        "tau_adp_in": tau_adp_in,
        "tau_m_in": tau_m_in,
    }


def reference(x_t, spk_t, mem_t_in, b_t_in, W_x2in_words, W_x2in_scales, b_x2in, W_rec4in_words, W_rec4in_scales, b_rec4in, W_out2in_words, W_out2in_scales, b_out2in, tau_adp_in, tau_m_in):
    spk = f64(spk_t)
    spk_out = spk[:, :R_OUT]
    spk_in = spk[:, R_OUT:]
    x = (mxq(f64(x_t), 1, "e4m3") @ unpack_weight(W_x2in_words, W_x2in_scales, FMT)) + f64(b_x2in)
    rec = (mxq(spk_in, 1, "e4m3") @ unpack_weight(W_rec4in_words, W_rec4in_scales, FMT)) + f64(b_rec4in)
    fbk = (mxq(spk_out, 1, "e4m3") @ unpack_weight(W_out2in_words, W_out2in_scales, FMT)) + f64(b_out2in)
    r_in_ = x + rec + fbk
    tau_m_s = sigmoid(f64(tau_m_in))
    tau_adp_s = sigmoid(f64(tau_adp_in))
    b = tau_adp_s * f64(b_t_in) + (1.0 - tau_adp_s) * spk_in
    new_thre = BASELINE_THRE + BETA * b
    mem = f64(mem_t_in) * tau_m_s + (1.0 - tau_m_s) * R_M * r_in_ - new_thre * spk_in * DT
    return mem

@@ -1,0 +1,284 @@
+from contextlib import ExitStack
+
+import concourse.mybir as mybir
+from concourse.masks import make_identity
+
+F32 = mybir.dt.float32
+BF16 = mybir.dt.bfloat16
+I32 = mybir.dt.int32
+U32 = mybir.dt.uint32
+U8 = mybir.dt.uint8
+FP8X4 = mybir.dt.float8_e4m3fn_x4
+ALU = mybir.AluOpType
+ACT = mybir.ActivationFunctionType
+
+P = 128
+SAMPLES = 4096
+NEURONS = 512
+CHUNK = 512
+ROW_TILES = CHUNK // P
+N_CHUNKS = SAMPLES // CHUNK
+BLOCKS = NEURONS // P
+PASSES = 4
+WORDS = 256
+HALVES = 2
+
+BASELINE_THRE = 0.1
+BETA = 1.8
+R_M = 3.0
+
+FLOPS = 2 * SAMPLES * (PASSES * 512) * NEURONS
+
+
+def tile_snnlayer_pa_t_kernel(
+    tc,
+    x_t,
+    spk_t,
+    mem_t_in,
+    b_t_in,
+    W_x2in_words,
+    W_x2in_scales,
+    b_x2in,
+    W_rec4in_words,
+    W_rec4in_scales,
+    b_rec4in,
+    W_out2in_words,
+    W_out2in_scales,
+    b_out2in,
+    tau_adp_in,
+    tau_m_in,
+    out,
+):
+    nc = tc.nc
+
+    x_chunks = x_t.rearrange("(c p i) k -> c p i k", p=P, i=ROW_TILES)
+    spk_chunks = spk_t.rearrange("(c p i) k -> c p i k", p=P, i=ROW_TILES)
+    mem_chunks = mem_t_in.rearrange("(c p i) n -> c p i n", p=P, i=ROW_TILES)
+    b_chunks = b_t_in.rearrange("(c p i) n -> c p i n", p=P, i=ROW_TILES)
+    out_chunks = out.rearrange("(c p i) n -> c p i n", p=P, i=ROW_TILES)
+
+    with ExitStack() as stack:
+        const = stack.enter_context(tc.tile_pool(name="const", bufs=1))
+        loads = stack.enter_context(tc.tile_pool(name="loads", bufs=3))
+        quant = stack.enter_context(tc.tile_pool(name="quant", bufs=2))
+        work = stack.enter_context(tc.tile_pool(name="work", bufs=3))
+        psum = stack.enter_context(tc.psum_pool(name="psum", bufs=2))
+        stack.enter_context(tc.manual_schedule())
+
+        x_tiles = {}
+        spk_tiles = {}
+        mem_tiles = {}
+        b_tiles = {}
+
+        def load_activations(c):
+            x_sb = loads.tile([P, ROW_TILES, 2 * 512], BF16, tag="x")
+            spk_sb = loads.tile([P, ROW_TILES, 2 * 512], BF16, tag="spk")
+            nc.sync.dma_start(out=x_sb[:], in_=x_chunks[c])
+            nc.sync.dma_start(out=spk_sb[:], in_=spk_chunks[c])
+            x_tiles[c] = x_sb
+            spk_tiles[c] = spk_sb
+
+        def load_state(c):
+            b_sb = loads.tile([P, ROW_TILES, NEURONS], BF16, tag="b")
+            mem_sb = loads.tile([P, ROW_TILES, NEURONS], BF16, tag="mem")
+            nc.sync.dma_start(out=b_sb[:], in_=b_chunks[c])
+            nc.sync.dma_start(out=mem_sb[:], in_=mem_chunks[c])
+            b_tiles[c] = b_sb
+            mem_tiles[c] = mem_sb
+
+        load_activations(0)
+
+        vectors = [b_x2in, b_rec4in, b_out2in, tau_adp_in, tau_m_in]
+        vec_rows = const.tile([P, P], BF16)
+        nc.vector.memset(vec_rows[:], 0.0)
+        for v, vector in enumerate(vectors):
+            nc.scalar.dma_start(
+                out=vec_rows[BLOCKS * v : BLOCKS * (v + 1), :], in_=vector.rearrange("(j m) -> j m", j=BLOCKS)
+            )
+        tau_m_rows = const.tile([P, NEURONS], BF16)
+        nc.scalar.dma_start(out=tau_m_rows[:], in_=tau_m_in.partition_broadcast(P))
+
+        w_words = const.tile([P, PASSES, NEURONS], I32, align_bytes=64)
+        w_planes = const.tile([P, PASSES, NEURONS], U8, align_bytes=64)
+        nc.vector.memset(w_planes[:].rearrange("p g n -> p (g n)").bitcast(I32), 0)
+        for quadrant in range(4):
+            rows = slice(4 * quadrant, 4 * quadrant + 4)
+            live = slice(32 * quadrant, 32 * quadrant + 4)
+            nc.sync.dma_start(
+                out=w_planes[live, 0:2, :].bitcast(I32),
+                in_=W_x2in_scales[:, rows, :].rearrange("g r n -> r g n").bitcast(I32),
+            )
+            nc.sync.dma_start(out=w_planes[live, 2, :].bitcast(I32), in_=W_out2in_scales[0, rows, :].bitcast(I32))
+            nc.sync.dma_start(out=w_planes[live, 3, :].bitcast(I32), in_=W_rec4in_scales[0, rows, :].bitcast(I32))
+        nc.sync.dma_start(
+            out=w_words[:, 0:2, :], in_=W_x2in_words.rearrange("g p n t -> p g (n t)").bitcast(I32)
+        )
+        nc.sync.dma_start(out=w_words[:, 2, :], in_=W_out2in_words[0].rearrange("p n t -> p (n t)").bitcast(I32))
+        nc.sync.dma_start(out=w_words[:, 3, :], in_=W_rec4in_words[0].rearrange("p n t -> p (n t)").bitcast(I32))
+        load_state(0)
+        load_activations(1)
+        load_state(1)
+
+        ident_bf16 = const.tile([P, P], BF16)
+        make_identity(nc, ident_bf16[:])
+        ident_f32 = const.tile([P, P], F32)
+        make_identity(nc, ident_f32[:])
+
+        vec_ps = psum.tile([P, 2, CHUNK], BF16, tag="bs")
+        nc.tensor.transpose(vec_ps[:, 0, 0:P], vec_rows[:], ident_bf16[:])
+        vec_cols = const.tile([P, len(vectors), BLOCKS], F32)
+        nc.vector.tensor_copy(
+            out=vec_cols[:].rearrange("p v j -> p (v j)"), in_=vec_ps[:, 0, 0 : len(vectors) * BLOCKS]
+        )
+        p_col = const.tile([P, BLOCKS], F32)
+        a_col = const.tile([P, BLOCKS], F32)
+        nc.scalar.activation(out=p_col[:], in_=vec_cols[:, 3, :], func=ACT.Sigmoid)
+        nc.scalar.activation(out=a_col[:], in_=vec_cols[:, 4, :], func=ACT.Sigmoid)
+
+        bias_two = const.tile([P, BLOCKS], F32)
+        bias_sum = const.tile([P, BLOCKS], F32)
+        nc.vector.tensor_tensor(out=bias_two[:], in0=vec_cols[:, 0, :], in1=vec_cols[:, 1, :], op=ALU.add)
+        nc.vector.tensor_tensor(out=bias_sum[:], in0=bias_two[:], in1=vec_cols[:, 2, :], op=ALU.add)
+        drive_gain = const.tile([P, BLOCKS], F32)
+        drive_bias = const.tile([P, BLOCKS], F32)
+        nc.vector.tensor_scalar(
+            out=drive_gain[:], in0=a_col[:], scalar1=-R_M, scalar2=R_M, op0=ALU.mult, op1=ALU.add
+        )
+        nc.vector.tensor_tensor(out=drive_bias[:], in0=drive_gain[:], in1=bias_sum[:], op=ALU.mult)
+        thre_b = const.tile([P, BLOCKS], F32)
+        thre_spk = const.tile([P, BLOCKS], F32)
+        nc.vector.tensor_scalar(out=thre_b[:], in0=p_col[:], scalar1=BETA, scalar2=None, op0=ALU.mult)
+        nc.vector.tensor_scalar(
+            out=thre_spk[:], in0=p_col[:], scalar1=-BETA, scalar2=BETA, op0=ALU.mult, op1=ALU.add
+        )
+        baseline = const.tile([P, 1], F32)
+        nc.vector.memset(baseline[:], BASELINE_THRE)
+        a_rows = const.tile([P, NEURONS], F32)
+
+        codes_tiles = {}
+        planes_tiles = {}
+        drive_tiles = {}
+        update_tiles = {}
+        decay_tiles = {}
+        out_tiles = {}
+
+        def transpose_and_quantise(c, half):
+            if half == 0:
+                codes_tiles[c] = quant.tile([P, PASSES, CHUNK], U32, tag="codes", name="codes", align_bytes=64)
+                planes_tiles[c] = quant.tile([P, PASSES, CHUNK], U8, tag="planes", name="planes", align_bytes=64)
+            source = (x_tiles[c] if half == 0 else spk_tiles[c])[:].bitcast(F32)
+            for g in (0, 1):
+                grouped = quant.tile([P, 4 * CHUNK], BF16, tag="grouped", bufs=4, align_bytes=64)
+                grouped_words = grouped[:].bitcast(F32).rearrange("p (s u) -> p s u", u=2)
+                for pair in range(ROW_TILES // 2):
+                    turned = psum.tile([P, 2, 2 * P], F32, tag="turned")
+                    for i in (0, 1):
+                        for u in (0, 1):
+                            nc.tensor.transpose(
+                                turned[:, u, P * i : P * (i + 1)],
+                                source[:, 2 * pair + i, WORDS * g + u : WORDS * (g + 1) : 2],
+                                ident_f32[:],
+                            )
+                    nc.scalar.copy(
+                        out=grouped_words[:, 2 * P * pair : 2 * P * (pair + 1), :],
+                        in_=turned[:].rearrange("p u s -> p s u"),
+                    )
+                nc.vector.quantize_mx(
+                    out=codes_tiles[c][:, 2 * half + g, :].bitcast(FP8X4),
+                    scales=planes_tiles[c][:, 2 * half + g, :],
+                    in_=grouped[:],
+                )
+
+        def drive(c, half):
+            for j in (2 * half, 2 * half + 1):
+                neurons = slice(P * j, P * (j + 1))
+                sums = psum.tile([P, CHUNK], F32, tag="sums")
+                for g in range(PASSES):
+                    nc.tensor.matmul_mx(
+                        out=sums[:],
+                        lhsT=w_words[:, g, neurons].bitcast(FP8X4),
+                        lhsT_scale=w_planes[:, g, neurons],
+                        rhs=codes_tiles[c][:, g, :].bitcast(FP8X4),
+                        rhs_scale=planes_tiles[c][:, g, :],
+                        start=(g == 0),
+                        stop=(g == PASSES - 1),
+                    )
+                driven = work.tile([P, CHUNK], F32, tag="driven", bufs=4)
+                nc.scalar.activation(
+                    out=driven[:],
+                    in_=sums[:],
+                    func=ACT.Identity,
+                    scale=drive_gain[:, j : j + 1],
+                    bias=drive_bias[:, j : j + 1],
+                )
+                drive_tiles[(c, j)] = driven
+
+        def threshold(c, half):
+            if half == 0:
+                update_tiles[c] = work.tile([P, BLOCKS, CHUNK], F32, tag="update", name="update", bufs=2)
+            for j in (2 * half, 2 * half + 1):
+                turned_bs = psum.tile([P, 2, CHUNK], BF16, tag="bs")
+                for i in range(ROW_TILES):
+                    samples = slice(P * i, P * (i + 1))
+                    nc.tensor.transpose(turned_bs[:, 0, samples], b_tiles[c][:, i, P * j : P * (j + 1)], ident_bf16[:])
+                    nc.tensor.transpose(
+                        turned_bs[:, 1, samples],
+                        spk_tiles[c][:, i, NEURONS + P * j : NEURONS + P * (j + 1)],
+                        ident_bf16[:],
+                    )
+                b_T = turned_bs[:, 0, :]
+                spk_T = turned_bs[:, 1, :]
+                thre_part = work.tile([P, CHUNK], F32, tag="thre_part")
+                nc.scalar.activation(
+                    out=thre_part[:], in_=b_T, func=ACT.Identity, scale=thre_b[:, j : j + 1], bias=baseline[:]
+                )
+                thre = work.tile([P, CHUNK], F32, tag="thre")
+                nc.vector.scalar_tensor_tensor(
+                    out=thre[:], in0=spk_T, scalar=thre_spk[:, j : j + 1], in1=thre_part[:], op0=ALU.mult, op1=ALU.add
+                )
+                reset = work.tile([P, CHUNK], F32, tag="reset")
+                nc.vector.tensor_tensor(out=reset[:], in0=thre[:], in1=spk_T, op=ALU.mult)
+                nc.vector.tensor_tensor(
+                    out=update_tiles[c][:, j, :], in0=drive_tiles[(c, j)][:], in1=reset[:], op=ALU.subtract
+                )
+
+        def decay(c):
+            decayed = work.tile([P, ROW_TILES, NEURONS], F32, tag="decayed", bufs=2)
+            nc.gpsimd.tensor_tensor(
+                out=decayed[:],
+                in0=mem_tiles[c][:],
+                in1=a_rows[:].unsqueeze(1).to_broadcast([P, ROW_TILES, NEURONS]),
+                op=ALU.mult,
+            )
+            decay_tiles[c] = decayed
+
+        def finish(c, half):
+            if half == 0:
+                out_tiles[c] = work.tile([P, ROW_TILES, NEURONS], F32, tag="result", name="result", bufs=2)
+            for i in (2 * half, 2 * half + 1):
+                back = psum.tile([P, NEURONS], F32, tag="back")
+                for j in range(BLOCKS):
+                    nc.tensor.transpose(
+                        back[:, P * j : P * (j + 1)], update_tiles[c][:, j, P * i : P * (i + 1)], ident_f32[:]
+                    )
+                nc.vector.tensor_tensor(out=out_tiles[c][:, i, :], in0=back[:], in1=decay_tiles[c][:, i, :], op=ALU.add)
+            if half == HALVES - 1:
+                nc.sync.dma_start(out=out_chunks[c], in_=out_tiles[c][:])
+
+        for half in range(HALVES):
+            transpose_and_quantise(0, half)
+        nc.scalar.activation(out=a_rows[:], in_=tau_m_rows[:], func=ACT.Sigmoid)
+        for c in range(N_CHUNKS + 1):
+            if c + 2 < N_CHUNKS:
+                load_activations(c + 2)
+                load_state(c + 2)
+            if c < N_CHUNKS:
+                decay(c)
+            for half in range(HALVES):
+                if c + 1 < N_CHUNKS:
+                    transpose_and_quantise(c + 1, half)
+                if c < N_CHUNKS:
+                    drive(c, half)
+                    threshold(c, half)
+                if c >= 1:
+                    finish(c - 1, half)

@@ -242,15 +242,13 @@ def tile_snnlayer_pa_t_kernel(
                     out=update_tiles[c][:, j, :], in0=drive_tiles[(c, j)][:], in1=reset[:], op=ALU.subtract
                 )
 
-        def decay(c):
-            decayed = work.tile([P, ROW_TILES, NEURONS], F32, tag="decayed", bufs=2)
-            nc.gpsimd.tensor_tensor(
-                out=decayed[:],
-                in0=mem_tiles[c][:],
-                in1=a_rows[:].unsqueeze(1).to_broadcast([P, ROW_TILES, NEURONS]),
-                op=ALU.mult,
-            )
-            decay_tiles[c] = decayed
+        def decay(c, half):
+            if half == 0:
+                decay_tiles[c] = work.tile([P, ROW_TILES, NEURONS], F32, tag="decayed", name="decayed", bufs=2)
+            for i in (2 * half, 2 * half + 1):
+                nc.gpsimd.tensor_tensor(
+                    out=decay_tiles[c][:, i, :], in0=mem_tiles[c][:, i, :], in1=a_rows[:], op=ALU.mult
+                )
 
         def finish(c, half):
             if half == 0:
@@ -272,12 +270,11 @@ def tile_snnlayer_pa_t_kernel(
             if c + 2 < N_CHUNKS:
                 load_activations(c + 2)
                 load_state(c + 2)
-            if c < N_CHUNKS:
-                decay(c)
             for half in range(HALVES):
                 if c + 1 < N_CHUNKS:
                     transpose_and_quantise(c + 1, half)
                 if c < N_CHUNKS:
+                    decay(c, half)
                     drive(c, half)
                     threshold(c, half)
                 if c >= 1:

@@ -61,8 +61,8 @@ def tile_snnlayer_pa_t_kernel(
         const = stack.enter_context(tc.tile_pool(name="const", bufs=1))
         loads = stack.enter_context(tc.tile_pool(name="loads", bufs=3))
         quant = stack.enter_context(tc.tile_pool(name="quant", bufs=2))
-        work = stack.enter_context(tc.tile_pool(name="work", bufs=3))
-        psum = stack.enter_context(tc.psum_pool(name="psum", bufs=2))
+        work = stack.enter_context(tc.tile_pool(name="work", bufs=4))
+        psum = stack.enter_context(tc.psum_pool(name="psum", bufs=8))
         stack.enter_context(tc.manual_schedule())
 
         x_tiles = {}
@@ -124,7 +124,7 @@ def tile_snnlayer_pa_t_kernel(
         ident_f32 = const.tile([P, P], F32)
         make_identity(nc, ident_f32[:])
 
-        vec_ps = psum.tile([P, 2, CHUNK], BF16, tag="bs")
+        vec_ps = psum.tile([P, 2, CHUNK], BF16, tag="bank")
         nc.tensor.transpose(vec_ps[:, 0, 0:P], vec_rows[:], ident_bf16[:])
         vec_cols = const.tile([P, len(vectors), BLOCKS], F32)
         nc.vector.tensor_copy(
@@ -171,7 +171,7 @@ def tile_snnlayer_pa_t_kernel(
                 grouped = quant.tile([P, 4 * CHUNK], BF16, tag="grouped", bufs=4, align_bytes=64)
                 grouped_words = grouped[:].bitcast(F32).rearrange("p (s u) -> p s u", u=2)
                 for pair in range(ROW_TILES // 2):
-                    turned = psum.tile([P, 2, 2 * P], F32, tag="turned")
+                    turned = psum.tile([P, 2, 2 * P], F32, tag="bank")
                     for i in (0, 1):
                         for u in (0, 1):
                             nc.tensor.transpose(
@@ -192,7 +192,7 @@ def tile_snnlayer_pa_t_kernel(
         def drive(c, half):
             for j in (2 * half, 2 * half + 1):
                 neurons = slice(P * j, P * (j + 1))
-                sums = psum.tile([P, CHUNK], F32, tag="sums")
+                sums = psum.tile([P, CHUNK], F32, tag="bank")
                 for g in range(PASSES):
                     nc.tensor.matmul_mx(
                         out=sums[:],
@@ -216,8 +216,14 @@ def tile_snnlayer_pa_t_kernel(
         def threshold(c, half):
             if half == 0:
                 update_tiles[c] = work.tile([P, BLOCKS, CHUNK], F32, tag="update", name="update", bufs=2)
-            for j in (2 * half, 2 * half + 1):
-                turned_bs = psum.tile([P, 2, CHUNK], BF16, tag="bs")
+            pair = (2 * half, 2 * half + 1)
+            b_T = {}
+            spk_T = {}
+            thre_part = {}
+            thre = {}
+            reset = {}
+            for j in pair:
+                turned_bs = psum.tile([P, 2, CHUNK], BF16, tag="bank")
                 for i in range(ROW_TILES):
                     samples = slice(P * i, P * (i + 1))
                     nc.tensor.transpose(turned_bs[:, 0, samples], b_tiles[c][:, i, P * j : P * (j + 1)], ident_bf16[:])
@@ -226,20 +232,29 @@ def tile_snnlayer_pa_t_kernel(
                         spk_tiles[c][:, i, NEURONS + P * j : NEURONS + P * (j + 1)],
                         ident_bf16[:],
                     )
-                b_T = turned_bs[:, 0, :]
-                spk_T = turned_bs[:, 1, :]
-                thre_part = work.tile([P, CHUNK], F32, tag="thre_part")
+                b_T[j] = turned_bs[:, 0, :]
+                spk_T[j] = turned_bs[:, 1, :]
+            for j in pair:
+                thre_part[j] = work.tile([P, CHUNK], F32, tag="thre_part", name="thre_part")
                 nc.scalar.activation(
-                    out=thre_part[:], in_=b_T, func=ACT.Identity, scale=thre_b[:, j : j + 1], bias=baseline[:]
+                    out=thre_part[j][:], in_=b_T[j], func=ACT.Identity, scale=thre_b[:, j : j + 1], bias=baseline[:]
                 )
-                thre = work.tile([P, CHUNK], F32, tag="thre")
+            for j in pair:
+                thre[j] = work.tile([P, CHUNK], F32, tag="thre", name="thre")
                 nc.vector.scalar_tensor_tensor(
-                    out=thre[:], in0=spk_T, scalar=thre_spk[:, j : j + 1], in1=thre_part[:], op0=ALU.mult, op1=ALU.add
+                    out=thre[j][:],
+                    in0=spk_T[j],
+                    scalar=thre_spk[:, j : j + 1],
+                    in1=thre_part[j][:],
+                    op0=ALU.mult,
+                    op1=ALU.add,
                 )
-                reset = work.tile([P, CHUNK], F32, tag="reset")
-                nc.vector.tensor_tensor(out=reset[:], in0=thre[:], in1=spk_T, op=ALU.mult)
+            for j in pair:
+                reset[j] = work.tile([P, CHUNK], F32, tag="reset", name="reset")
+                nc.vector.tensor_tensor(out=reset[j][:], in0=thre[j][:], in1=spk_T[j], op=ALU.mult)
+            for j in pair:
                 nc.vector.tensor_tensor(
-                    out=update_tiles[c][:, j, :], in0=drive_tiles[(c, j)][:], in1=reset[:], op=ALU.subtract
+                    out=update_tiles[c][:, j, :], in0=drive_tiles[(c, j)][:], in1=reset[j][:], op=ALU.subtract
                 )
 
         def decay(c, half):
@@ -254,7 +269,7 @@ def tile_snnlayer_pa_t_kernel(
             if half == 0:
                 out_tiles[c] = work.tile([P, ROW_TILES, NEURONS], F32, tag="result", name="result", bufs=2)
             for i in (2 * half, 2 * half + 1):
-                back = psum.tile([P, NEURONS], F32, tag="back")
+                back = psum.tile([P, NEURONS], F32, tag="bank")
                 for j in range(BLOCKS):
                     nc.tensor.transpose(
                         back[:, P * j : P * (j + 1)], update_tiles[c][:, j, P * i : P * (i + 1)], ident_f32[:]

@@ -21,7 +21,10 @@ N_CHUNKS = SAMPLES // CHUNK
 BLOCKS = NEURONS // P
 PASSES = 4
 WORDS = 256
-HALVES = 2
+STEPS = 4
+UNITS = N_CHUNKS * STEPS
+assert PASSES == STEPS and BLOCKS == STEPS and ROW_TILES == STEPS
+FINISH_LAG = STEPS + 1
 
 BASELINE_THRE = 0.1
 BETA = 1.8
@@ -158,139 +161,126 @@ def tile_snnlayer_pa_t_kernel(
         codes_tiles = {}
         planes_tiles = {}
         drive_tiles = {}
+        spk_T_tiles = {}
+        thre_tiles = {}
         update_tiles = {}
         decay_tiles = {}
-        out_tiles = {}
 
-        def transpose_and_quantise(c, half):
-            if half == 0:
+        def turn_and_quantise(c, g):
+            if g == 0:
                 codes_tiles[c] = quant.tile([P, PASSES, CHUNK], U32, tag="codes", name="codes", align_bytes=64)
                 planes_tiles[c] = quant.tile([P, PASSES, CHUNK], U8, tag="planes", name="planes", align_bytes=64)
-            source = (x_tiles[c] if half == 0 else spk_tiles[c])[:].bitcast(F32)
-            for g in (0, 1):
-                grouped = quant.tile([P, 4 * CHUNK], BF16, tag="grouped", bufs=4, align_bytes=64)
-                grouped_words = grouped[:].bitcast(F32).rearrange("p (s u) -> p s u", u=2)
-                for pair in range(ROW_TILES // 2):
-                    turned = psum.tile([P, 2, 2 * P], F32, tag="bank")
-                    for i in (0, 1):
-                        for u in (0, 1):
-                            nc.tensor.transpose(
-                                turned[:, u, P * i : P * (i + 1)],
-                                source[:, 2 * pair + i, WORDS * g + u : WORDS * (g + 1) : 2],
-                                ident_f32[:],
-                            )
-                    nc.scalar.copy(
-                        out=grouped_words[:, 2 * P * pair : 2 * P * (pair + 1), :],
-                        in_=turned[:].rearrange("p u s -> p s u"),
-                    )
-                nc.vector.quantize_mx(
-                    out=codes_tiles[c][:, 2 * half + g, :].bitcast(FP8X4),
-                    scales=planes_tiles[c][:, 2 * half + g, :],
-                    in_=grouped[:],
+            source = (x_tiles[c] if g < 2 else spk_tiles[c])[:].bitcast(F32)
+            first_word = WORDS * (g % 2)
+            grouped = quant.tile([P, 4 * CHUNK], BF16, tag="grouped", bufs=3, align_bytes=64)
+            grouped_words = grouped[:].bitcast(F32).rearrange("p (s u) -> p s u", u=2)
+            for bank in range(ROW_TILES // 2):
+                turned = psum.tile([P, 2, 2 * P], F32, tag="bank")
+                for i in (0, 1):
+                    for u in (0, 1):
+                        nc.tensor.transpose(
+                            turned[:, u, P * i : P * (i + 1)],
+                            source[:, 2 * bank + i, first_word + u : first_word + WORDS : 2],
+                            ident_f32[:],
+                        )
+                nc.scalar.copy(
+                    out=grouped_words[:, 2 * P * bank : 2 * P * (bank + 1), :],
+                    in_=turned[:].rearrange("p u s -> p s u"),
                 )
+            nc.vector.quantize_mx(
+                out=codes_tiles[c][:, g, :].bitcast(FP8X4), scales=planes_tiles[c][:, g, :], in_=grouped[:]
+            )
 
-        def drive(c, half):
-            for j in (2 * half, 2 * half + 1):
-                neurons = slice(P * j, P * (j + 1))
-                sums = psum.tile([P, CHUNK], F32, tag="bank")
-                for g in range(PASSES):
-                    nc.tensor.matmul_mx(
-                        out=sums[:],
-                        lhsT=w_words[:, g, neurons].bitcast(FP8X4),
-                        lhsT_scale=w_planes[:, g, neurons],
-                        rhs=codes_tiles[c][:, g, :].bitcast(FP8X4),
-                        rhs_scale=planes_tiles[c][:, g, :],
-                        start=(g == 0),
-                        stop=(g == PASSES - 1),
-                    )
-                driven = work.tile([P, CHUNK], F32, tag="driven", bufs=4)
-                nc.scalar.activation(
-                    out=driven[:],
-                    in_=sums[:],
-                    func=ACT.Identity,
-                    scale=drive_gain[:, j : j + 1],
-                    bias=drive_bias[:, j : j + 1],
-                )
-                drive_tiles[(c, j)] = driven
+        def decay(c, i):
+            decayed = work.tile([P, NEURONS], F32, tag="decayed", bufs=8)
+            nc.gpsimd.tensor_tensor(out=decayed[:], in0=mem_tiles[c][:, i, :], in1=a_rows[:], op=ALU.mult)
+            decay_tiles[(c, i)] = decayed
 
-        def threshold(c, half):
-            if half == 0:
-                update_tiles[c] = work.tile([P, BLOCKS, CHUNK], F32, tag="update", name="update", bufs=2)
-            pair = (2 * half, 2 * half + 1)
-            b_T = {}
-            spk_T = {}
-            thre_part = {}
-            thre = {}
-            reset = {}
-            for j in pair:
-                turned_bs = psum.tile([P, 2, CHUNK], BF16, tag="bank")
-                for i in range(ROW_TILES):
-                    samples = slice(P * i, P * (i + 1))
-                    nc.tensor.transpose(turned_bs[:, 0, samples], b_tiles[c][:, i, P * j : P * (j + 1)], ident_bf16[:])
-                    nc.tensor.transpose(
-                        turned_bs[:, 1, samples],
-                        spk_tiles[c][:, i, NEURONS + P * j : NEURONS + P * (j + 1)],
-                        ident_bf16[:],
-                    )
-                b_T[j] = turned_bs[:, 0, :]
-                spk_T[j] = turned_bs[:, 1, :]
-            for j in pair:
-                thre_part[j] = work.tile([P, CHUNK], F32, tag="thre_part", name="thre_part")
-                nc.scalar.activation(
-                    out=thre_part[j][:], in_=b_T[j], func=ACT.Identity, scale=thre_b[:, j : j + 1], bias=baseline[:]
+        def drive(c, j):
+            neurons = slice(P * j, P * (j + 1))
+            sums = psum.tile([P, CHUNK], F32, tag="bank")
+            for g in range(PASSES):
+                nc.tensor.matmul_mx(
+                    out=sums[:],
+                    lhsT=w_words[:, g, neurons].bitcast(FP8X4),
+                    lhsT_scale=w_planes[:, g, neurons],
+                    rhs=codes_tiles[c][:, g, :].bitcast(FP8X4),
+                    rhs_scale=planes_tiles[c][:, g, :],
+                    start=(g == 0),
+                    stop=(g == PASSES - 1),
                 )
-            for j in pair:
-                thre[j] = work.tile([P, CHUNK], F32, tag="thre", name="thre")
-                nc.vector.scalar_tensor_tensor(
-                    out=thre[j][:],
-                    in0=spk_T[j],
-                    scalar=thre_spk[:, j : j + 1],
-                    in1=thre_part[j][:],
-                    op0=ALU.mult,
-                    op1=ALU.add,
-                )
-            for j in pair:
-                reset[j] = work.tile([P, CHUNK], F32, tag="reset", name="reset")
-                nc.vector.tensor_tensor(out=reset[j][:], in0=thre[j][:], in1=spk_T[j], op=ALU.mult)
-            for j in pair:
-                nc.vector.tensor_tensor(
-                    out=update_tiles[c][:, j, :], in0=drive_tiles[(c, j)][:], in1=reset[j][:], op=ALU.subtract
-                )
+            driven = work.tile([P, CHUNK], F32, tag="driven")
+            nc.scalar.activation(
+                out=driven[:],
+                in_=sums[:],
+                func=ACT.Identity,
+                scale=drive_gain[:, j : j + 1],
+                bias=drive_bias[:, j : j + 1],
+            )
+            drive_tiles[(c, j)] = driven
 
-        def decay(c, half):
-            if half == 0:
-                decay_tiles[c] = work.tile([P, ROW_TILES, NEURONS], F32, tag="decayed", name="decayed", bufs=2)
-            for i in (2 * half, 2 * half + 1):
-                nc.gpsimd.tensor_tensor(
-                    out=decay_tiles[c][:, i, :], in0=mem_tiles[c][:, i, :], in1=a_rows[:], op=ALU.mult
+        def threshold(c, j):
+            turned_bs = psum.tile([P, 2, CHUNK], BF16, tag="bank")
+            for i in range(ROW_TILES):
+                samples = slice(P * i, P * (i + 1))
+                nc.tensor.transpose(turned_bs[:, 0, samples], b_tiles[c][:, i, P * j : P * (j + 1)], ident_bf16[:])
+                nc.tensor.transpose(
+                    turned_bs[:, 1, samples],
+                    spk_tiles[c][:, i, NEURONS + P * j : NEURONS + P * (j + 1)],
+                    ident_bf16[:],
                 )
+            thre_part = work.tile([P, CHUNK], F32, tag="thre_part")
+            nc.scalar.activation(
+                out=thre_part[:],
+                in_=turned_bs[:, 0, :],
+                func=ACT.Identity,
+                scale=thre_b[:, j : j + 1],
+                bias=baseline[:],
+            )
+            thre = work.tile([P, CHUNK], F32, tag="thre")
+            nc.vector.scalar_tensor_tensor(
+                out=thre[:],
+                in0=turned_bs[:, 1, :],
+                scalar=thre_spk[:, j : j + 1],
+                in1=thre_part[:],
+                op0=ALU.mult,
+                op1=ALU.add,
+            )
+            spk_T_tiles[(c, j)] = turned_bs[:, 1, :]
+            thre_tiles[(c, j)] = thre
 
-        def finish(c, half):
-            if half == 0:
-                out_tiles[c] = work.tile([P, ROW_TILES, NEURONS], F32, tag="result", name="result", bufs=2)
-            for i in (2 * half, 2 * half + 1):
-                back = psum.tile([P, NEURONS], F32, tag="bank")
-                for j in range(BLOCKS):
-                    nc.tensor.transpose(
-                        back[:, P * j : P * (j + 1)], update_tiles[c][:, j, P * i : P * (i + 1)], ident_f32[:]
-                    )
-                nc.vector.tensor_tensor(out=out_tiles[c][:, i, :], in0=back[:], in1=decay_tiles[c][:, i, :], op=ALU.add)
-            if half == HALVES - 1:
-                nc.sync.dma_start(out=out_chunks[c], in_=out_tiles[c][:])
+        def reset_and_update(c, j):
+            reset = work.tile([P, CHUNK], F32, tag="reset")
+            nc.vector.tensor_tensor(out=reset[:], in0=thre_tiles[(c, j)][:], in1=spk_T_tiles[(c, j)], op=ALU.mult)
+            update = work.tile([P, CHUNK], F32, tag="update", bufs=2 * STEPS)
+            nc.gpsimd.tensor_tensor(out=update[:], in0=drive_tiles[(c, j)][:], in1=reset[:], op=ALU.subtract)
+            update_tiles[(c, j)] = update
 
-        for half in range(HALVES):
-            transpose_and_quantise(0, half)
+        def finish(c, i):
+            back = psum.tile([P, NEURONS], F32, tag="bank")
+            for j in range(BLOCKS):
+                nc.tensor.transpose(
+                    back[:, P * j : P * (j + 1)], update_tiles[(c, j)][:, P * i : P * (i + 1)], ident_f32[:]
+                )
+            result = work.tile([P, NEURONS], F32, tag="result")
+            nc.vector.tensor_tensor(out=result[:], in0=back[:], in1=decay_tiles[(c, i)][:], op=ALU.add)
+            nc.sync.dma_start(out=out_chunks[c][:, i, :], in_=result[:])
+
+        for g in range(PASSES):
+            turn_and_quantise(0, g)
         nc.scalar.activation(out=a_rows[:], in_=tau_m_rows[:], func=ACT.Sigmoid)
-        for c in range(N_CHUNKS + 1):
-            if c + 2 < N_CHUNKS:
+        for n in range(UNITS + FINISH_LAG):
+            c, q = divmod(n, STEPS)
+            if q == 0 and c + 2 < N_CHUNKS:
                 load_activations(c + 2)
                 load_state(c + 2)
-            for half in range(HALVES):
-                if c + 1 < N_CHUNKS:
-                    transpose_and_quantise(c + 1, half)
-                if c < N_CHUNKS:
-                    decay(c, half)
-                    drive(c, half)
-                    threshold(c, half)
-                if c >= 1:
-                    finish(c - 1, half)
+            if c + 1 < N_CHUNKS:
+                turn_and_quantise(c + 1, q)
+            if n < UNITS:
+                decay(c, q)
+                drive(c, q)
+                threshold(c, q)
+            if n >= FINISH_LAG:
+                finish(*divmod(n - FINISH_LAG, STEPS))
+            if n < UNITS:
+                reset_and_update(c, q)

@@ -24,6 +24,8 @@ WORDS = 256
 STEPS = 4
 UNITS = N_CHUNKS * STEPS
 assert PASSES == STEPS and BLOCKS == STEPS and ROW_TILES == STEPS
+TURN_LEAD = STEPS
+THRE_LEAD = 2
 FINISH_LAG = STEPS + 1
 
 BASELINE_THRE = 0.1
@@ -65,7 +67,7 @@ def tile_snnlayer_pa_t_kernel(
         loads = stack.enter_context(tc.tile_pool(name="loads", bufs=3))
         quant = stack.enter_context(tc.tile_pool(name="quant", bufs=2))
         work = stack.enter_context(tc.tile_pool(name="work", bufs=4))
-        psum = stack.enter_context(tc.psum_pool(name="psum", bufs=8))
+        psum = stack.enter_context(tc.psum_pool(name="psum", bufs=2))
         stack.enter_context(tc.manual_schedule())
 
         x_tiles = {}
@@ -73,33 +75,31 @@ def tile_snnlayer_pa_t_kernel(
         mem_tiles = {}
         b_tiles = {}
 
-        def load_activations(c):
-            x_sb = loads.tile([P, ROW_TILES, 2 * 512], BF16, tag="x")
-            spk_sb = loads.tile([P, ROW_TILES, 2 * 512], BF16, tag="spk")
-            nc.sync.dma_start(out=x_sb[:], in_=x_chunks[c])
-            nc.sync.dma_start(out=spk_sb[:], in_=spk_chunks[c])
-            x_tiles[c] = x_sb
-            spk_tiles[c] = spk_sb
+        def load_spk(c):
+            spk_tiles[c] = loads.tile([P, ROW_TILES, 2 * 512], BF16, tag="spk", name="spk_sb")
+            nc.sync.dma_start(out=spk_tiles[c][:], in_=spk_chunks[c])
 
-        def load_state(c):
-            b_sb = loads.tile([P, ROW_TILES, NEURONS], BF16, tag="b")
-            mem_sb = loads.tile([P, ROW_TILES, NEURONS], BF16, tag="mem")
-            nc.sync.dma_start(out=b_sb[:], in_=b_chunks[c])
-            nc.sync.dma_start(out=mem_sb[:], in_=mem_chunks[c])
-            b_tiles[c] = b_sb
-            mem_tiles[c] = mem_sb
+        def load_x(c):
+            x_tiles[c] = loads.tile([P, ROW_TILES, 2 * 512], BF16, tag="x", name="x_sb")
+            nc.sync.dma_start(out=x_tiles[c][:], in_=x_chunks[c])
 
-        load_activations(0)
+        def load_b(c):
+            b_tiles[c] = loads.tile([P, ROW_TILES, NEURONS], BF16, tag="b", name="b_sb")
+            nc.sync.dma_start(out=b_tiles[c][:], in_=b_chunks[c])
+
+        def load_mem(c):
+            mem_tiles[c] = loads.tile([P, ROW_TILES, NEURONS], BF16, tag="mem", name="mem_sb")
+            nc.sync.dma_start(out=mem_tiles[c][:], in_=mem_chunks[c])
+
+        load_spk(0)
+        load_b(0)
+        load_x(0)
 
         vectors = [b_x2in, b_rec4in, b_out2in, tau_adp_in, tau_m_in]
-        vec_rows = const.tile([P, P], BF16)
+        vec_rows = const.tile([P, NEURONS], BF16)
         nc.vector.memset(vec_rows[:], 0.0)
         for v, vector in enumerate(vectors):
-            nc.scalar.dma_start(
-                out=vec_rows[BLOCKS * v : BLOCKS * (v + 1), :], in_=vector.rearrange("(j m) -> j m", j=BLOCKS)
-            )
-        tau_m_rows = const.tile([P, NEURONS], BF16)
-        nc.scalar.dma_start(out=tau_m_rows[:], in_=tau_m_in.partition_broadcast(P))
+            nc.scalar.dma_start(out=vec_rows[v : v + 1, :], in_=vector.rearrange("(o n) -> o n", o=1))
 
         w_words = const.tile([P, PASSES, NEURONS], I32, align_bytes=64)
         w_planes = const.tile([P, PASSES, NEURONS], U8, align_bytes=64)
@@ -107,36 +107,48 @@ def tile_snnlayer_pa_t_kernel(
         for quadrant in range(4):
             rows = slice(4 * quadrant, 4 * quadrant + 4)
             live = slice(32 * quadrant, 32 * quadrant + 4)
+            nc.sync.dma_start(out=w_planes[live, 0, :].bitcast(I32), in_=W_rec4in_scales[0, rows, :].bitcast(I32))
+            nc.sync.dma_start(out=w_planes[live, 1, :].bitcast(I32), in_=W_out2in_scales[0, rows, :].bitcast(I32))
             nc.sync.dma_start(
-                out=w_planes[live, 0:2, :].bitcast(I32),
+                out=w_planes[live, 2:4, :].bitcast(I32),
                 in_=W_x2in_scales[:, rows, :].rearrange("g r n -> r g n").bitcast(I32),
             )
-            nc.sync.dma_start(out=w_planes[live, 2, :].bitcast(I32), in_=W_out2in_scales[0, rows, :].bitcast(I32))
-            nc.sync.dma_start(out=w_planes[live, 3, :].bitcast(I32), in_=W_rec4in_scales[0, rows, :].bitcast(I32))
+        nc.sync.dma_start(out=w_words[:, 0, :], in_=W_rec4in_words[0].rearrange("p n t -> p (n t)").bitcast(I32))
+        nc.sync.dma_start(out=w_words[:, 1, :], in_=W_out2in_words[0].rearrange("p n t -> p (n t)").bitcast(I32))
         nc.sync.dma_start(
-            out=w_words[:, 0:2, :], in_=W_x2in_words.rearrange("g p n t -> p g (n t)").bitcast(I32)
+            out=w_words[:, 2:4, :], in_=W_x2in_words.rearrange("g p n t -> p g (n t)").bitcast(I32)
         )
-        nc.sync.dma_start(out=w_words[:, 2, :], in_=W_out2in_words[0].rearrange("p n t -> p (n t)").bitcast(I32))
-        nc.sync.dma_start(out=w_words[:, 3, :], in_=W_rec4in_words[0].rearrange("p n t -> p (n t)").bitcast(I32))
-        load_state(0)
-        load_activations(1)
-        load_state(1)
+        load_mem(0)
+        load_spk(1)
+        load_b(1)
+        load_x(1)
+        load_mem(1)
 
-        ident_bf16 = const.tile([P, P], BF16)
-        make_identity(nc, ident_bf16[:])
         ident_f32 = const.tile([P, P], F32)
         make_identity(nc, ident_f32[:])
+        ident_bf16 = const.tile([P, P], BF16)
+        make_identity(nc, ident_bf16[:])
 
-        vec_ps = psum.tile([P, 2, CHUNK], BF16, tag="bank")
-        nc.tensor.transpose(vec_ps[:, 0, 0:P], vec_rows[:], ident_bf16[:])
-        vec_cols = const.tile([P, len(vectors), BLOCKS], F32)
-        nc.vector.tensor_copy(
-            out=vec_cols[:].rearrange("p v j -> p (v j)"), in_=vec_ps[:, 0, 0 : len(vectors) * BLOCKS]
+        vec_ps = psum.tile([P, 2, P], F32, tag="turned", bufs=3)
+        vec_words = vec_rows[:].bitcast(F32)
+        for u in (0, 1):
+            nc.tensor.transpose(vec_ps[:, u, :], vec_words[:, u:WORDS:2], ident_f32[:])
+        tau_ps = psum.tile([P, NEURONS], F32, tag="sums")
+        nc.tensor.matmul(
+            tau_ps[:], lhsT=ident_bf16[:, 4:5].to_broadcast([P, P]), rhs=vec_rows[:], start=True, stop=True
         )
+        vec_cols = const.tile([P, len(vectors), BLOCKS], F32)
+        for u in (0, 1):
+            nc.vector.tensor_copy(
+                out=vec_cols[:, :, 2 * u : 2 * u + 2],
+                in_=vec_ps[:, u, :].bitcast(BF16).rearrange("p (v e) -> p v e", e=2)[:, 0 : len(vectors), :],
+            )
         p_col = const.tile([P, BLOCKS], F32)
         a_col = const.tile([P, BLOCKS], F32)
         nc.scalar.activation(out=p_col[:], in_=vec_cols[:, 3, :], func=ACT.Sigmoid)
         nc.scalar.activation(out=a_col[:], in_=vec_cols[:, 4, :], func=ACT.Sigmoid)
+        a_rows = const.tile([P, NEURONS], F32)
+        nc.scalar.activation(out=a_rows[:], in_=tau_ps[:], func=ACT.Sigmoid)
 
         bias_two = const.tile([P, BLOCKS], F32)
         bias_sum = const.tile([P, BLOCKS], F32)
@@ -154,28 +166,42 @@ def tile_snnlayer_pa_t_kernel(
         nc.vector.tensor_scalar(
             out=thre_spk[:], in0=p_col[:], scalar1=-BETA, scalar2=BETA, op0=ALU.mult, op1=ALU.add
         )
-        baseline = const.tile([P, 1], F32)
-        nc.vector.memset(baseline[:], BASELINE_THRE)
-        a_rows = const.tile([P, NEURONS], F32)
 
+        w_codes = const.tile([P, PASSES, NEURONS], I32, align_bytes=64)
+        w_scales = const.tile([P, PASSES, NEURONS], U8, align_bytes=64)
+
+        def permute_scales():
+            nc.vector.tensor_copy(
+                out=w_scales[:].rearrange("p g (j m) -> p g m j", j=BLOCKS),
+                in_=w_planes[:].rearrange("p g (m j) -> p g m j", j=BLOCKS),
+            )
+
+        def permute_words(g):
+            nc.vector.tensor_copy(
+                out=w_codes[:, g, :].rearrange("p (j m) -> p j m", j=BLOCKS),
+                in_=w_words[:, g, :].rearrange("p (m j) -> p j m", j=BLOCKS),
+            )
+
+        turned_tiles = {}
+        grouped_tiles = {}
         codes_tiles = {}
         planes_tiles = {}
-        drive_tiles = {}
-        spk_T_tiles = {}
+        b_turned_tiles = {}
+        sums_tiles = {}
+        spk_part_tiles = {}
         thre_tiles = {}
+        reset_tiles = {}
+        offset_tiles = {}
         update_tiles = {}
         decay_tiles = {}
+        back_tiles = {}
 
-        def turn_and_quantise(c, g):
-            if g == 0:
-                codes_tiles[c] = quant.tile([P, PASSES, CHUNK], U32, tag="codes", name="codes", align_bytes=64)
-                planes_tiles[c] = quant.tile([P, PASSES, CHUNK], U8, tag="planes", name="planes", align_bytes=64)
-            source = (x_tiles[c] if g < 2 else spk_tiles[c])[:].bitcast(F32)
-            first_word = WORDS * (g % 2)
-            grouped = quant.tile([P, 4 * CHUNK], BF16, tag="grouped", bufs=3, align_bytes=64)
-            grouped_words = grouped[:].bitcast(F32).rearrange("p (s u) -> p s u", u=2)
+        def turn(k):
+            c, g = divmod(k, PASSES)
+            source = (spk_tiles[c] if g < 2 else x_tiles[c])[:].bitcast(F32)
+            first_word = (WORDS, 0, 0, WORDS)[g]
             for bank in range(ROW_TILES // 2):
-                turned = psum.tile([P, 2, 2 * P], F32, tag="bank")
+                turned = psum.tile([P, 2, 2 * P], F32, tag="turned", bufs=3, name="turned")
                 for i in (0, 1):
                     for u in (0, 1):
                         nc.tensor.transpose(
@@ -183,104 +209,172 @@ def tile_snnlayer_pa_t_kernel(
                             source[:, 2 * bank + i, first_word + u : first_word + WORDS : 2],
                             ident_f32[:],
                         )
+                turned_tiles[(k, bank)] = turned
+
+        def group(k):
+            spike = k % PASSES == 0
+            grouped = quant.tile(
+                [P, 4 * CHUNK], BF16, tag="grouped_in" if spike else "grouped", bufs=3, name="grouped", align_bytes=64
+            )
+            words = grouped[:].bitcast(F32).rearrange("p (s u) -> p s u", u=2)
+            for bank in range(ROW_TILES // 2):
                 nc.scalar.copy(
-                    out=grouped_words[:, 2 * P * bank : 2 * P * (bank + 1), :],
-                    in_=turned[:].rearrange("p u s -> p s u"),
+                    out=words[:, 2 * P * bank : 2 * P * (bank + 1), :],
+                    in_=turned_tiles[(k, bank)][:].rearrange("p u s -> p s u"),
                 )
+            grouped_tiles[k] = grouped
+
+        def quantise(k):
+            c, g = divmod(k, PASSES)
+            if g == 0:
+                codes_tiles[c] = quant.tile([P, PASSES, CHUNK], U32, tag="codes", name="codes", align_bytes=64)
+                planes_tiles[c] = quant.tile([P, PASSES, CHUNK], U8, tag="planes", name="planes", align_bytes=64)
             nc.vector.quantize_mx(
-                out=codes_tiles[c][:, g, :].bitcast(FP8X4), scales=planes_tiles[c][:, g, :], in_=grouped[:]
+                out=codes_tiles[c][:, g, :].bitcast(FP8X4), scales=planes_tiles[c][:, g, :], in_=grouped_tiles[k][:]
             )
 
-        def decay(c, i):
-            decayed = work.tile([P, NEURONS], F32, tag="decayed", bufs=8)
-            nc.gpsimd.tensor_tensor(out=decayed[:], in0=mem_tiles[c][:, i, :], in1=a_rows[:], op=ALU.mult)
-            decay_tiles[(c, i)] = decayed
+        def spikes(k):
+            c, j = divmod(k, BLOCKS)
+            return grouped_tiles[PASSES * c][:].rearrange("p (s t) -> p t s", t=4)[:, j, :]
 
-        def drive(c, j):
+        def turn_b(c, u):
+            turned = psum.tile([P, CHUNK], F32, tag="b_turned", name="b_turned")
+            source = b_tiles[c][:].bitcast(F32)
+            for i in range(ROW_TILES):
+                nc.tensor.transpose(turned[:, P * i : P * (i + 1)], source[:, i, u:WORDS:2], ident_f32[:])
+            b_turned_tiles[(c, u)] = turned
+
+        def spike_part(k):
+            j = k % BLOCKS
+            part = work.tile([P, CHUNK], F32, tag="spk_part", name="spk_part")
+            nc.scalar.activation(out=part[:], in_=spikes(k), func=ACT.Identity, scale=thre_spk[:, j : j + 1])
+            spk_part_tiles[k] = part
+
+        def threshold(k):
+            c, j = divmod(k, BLOCKS)
+            turned = b_turned_tiles[(c, j // 2)][:].bitcast(BF16).rearrange("p (s e) -> p e s", e=2)
+            thre = work.tile([P, CHUNK], F32, tag="thre", name="thre")
+            nc.vector.scalar_tensor_tensor(
+                out=thre[:],
+                in0=turned[:, j % 2, :],
+                scalar=thre_b[:, j : j + 1],
+                in1=spk_part_tiles[k][:],
+                op0=ALU.mult,
+                op1=ALU.add,
+            )
+            thre_tiles[k] = thre
+
+        def reset(k):
+            product = work.tile([P, CHUNK], F32, tag="reset", name="reset")
+            nc.vector.scalar_tensor_tensor(
+                out=product[:], in0=thre_tiles[k][:], scalar=BASELINE_THRE, in1=spikes(k), op0=ALU.add, op1=ALU.mult
+            )
+            reset_tiles[k] = product
+
+        def offset(k):
+            j = k % BLOCKS
+            part = work.tile([P, CHUNK], F32, tag="offset", name="offset")
+            nc.scalar.activation(
+                out=part[:], in_=reset_tiles[k][:], func=ACT.Identity, scale=-1.0, bias=drive_bias[:, j : j + 1]
+            )
+            offset_tiles[k] = part
+
+        def matmuls(k):
+            c, j = divmod(k, BLOCKS)
             neurons = slice(P * j, P * (j + 1))
-            sums = psum.tile([P, CHUNK], F32, tag="bank")
+            sums = psum.tile([P, CHUNK], F32, tag="sums", name="sums")
             for g in range(PASSES):
                 nc.tensor.matmul_mx(
                     out=sums[:],
-                    lhsT=w_words[:, g, neurons].bitcast(FP8X4),
-                    lhsT_scale=w_planes[:, g, neurons],
+                    lhsT=w_codes[:, g, neurons].bitcast(FP8X4),
+                    lhsT_scale=w_scales[:, g, neurons],
                     rhs=codes_tiles[c][:, g, :].bitcast(FP8X4),
                     rhs_scale=planes_tiles[c][:, g, :],
                     start=(g == 0),
                     stop=(g == PASSES - 1),
                 )
-            driven = work.tile([P, CHUNK], F32, tag="driven")
-            nc.scalar.activation(
-                out=driven[:],
-                in_=sums[:],
-                func=ACT.Identity,
-                scale=drive_gain[:, j : j + 1],
-                bias=drive_bias[:, j : j + 1],
-            )
-            drive_tiles[(c, j)] = driven
+            sums_tiles[k] = sums
 
-        def threshold(c, j):
-            turned_bs = psum.tile([P, 2, CHUNK], BF16, tag="bank")
-            for i in range(ROW_TILES):
-                samples = slice(P * i, P * (i + 1))
-                nc.tensor.transpose(turned_bs[:, 0, samples], b_tiles[c][:, i, P * j : P * (j + 1)], ident_bf16[:])
-                nc.tensor.transpose(
-                    turned_bs[:, 1, samples],
-                    spk_tiles[c][:, i, NEURONS + P * j : NEURONS + P * (j + 1)],
-                    ident_bf16[:],
-                )
-            thre_part = work.tile([P, CHUNK], F32, tag="thre_part")
-            nc.scalar.activation(
-                out=thre_part[:],
-                in_=turned_bs[:, 0, :],
-                func=ACT.Identity,
-                scale=thre_b[:, j : j + 1],
-                bias=baseline[:],
-            )
-            thre = work.tile([P, CHUNK], F32, tag="thre")
+        def update(k):
+            j = k % BLOCKS
+            part = work.tile([P, CHUNK], F32, tag="update", bufs=10, name="update")
             nc.vector.scalar_tensor_tensor(
-                out=thre[:],
-                in0=turned_bs[:, 1, :],
-                scalar=thre_spk[:, j : j + 1],
-                in1=thre_part[:],
+                out=part[:],
+                in0=sums_tiles[k][:],
+                scalar=drive_gain[:, j : j + 1],
+                in1=offset_tiles[k][:],
                 op0=ALU.mult,
                 op1=ALU.add,
             )
-            spk_T_tiles[(c, j)] = turned_bs[:, 1, :]
-            thre_tiles[(c, j)] = thre
+            update_tiles[k] = part
 
-        def reset_and_update(c, j):
-            reset = work.tile([P, CHUNK], F32, tag="reset")
-            nc.vector.tensor_tensor(out=reset[:], in0=thre_tiles[(c, j)][:], in1=spk_T_tiles[(c, j)], op=ALU.mult)
-            update = work.tile([P, CHUNK], F32, tag="update", bufs=2 * STEPS)
-            nc.gpsimd.tensor_tensor(out=update[:], in0=drive_tiles[(c, j)][:], in1=reset[:], op=ALU.subtract)
-            update_tiles[(c, j)] = update
+        def decay(k):
+            c, i = divmod(k, ROW_TILES)
+            decayed = work.tile([P, NEURONS], F32, tag="decayed", bufs=8, name="decayed")
+            nc.gpsimd.tensor_tensor(out=decayed[:], in0=mem_tiles[c][:, i, :], in1=a_rows[:], op=ALU.mult)
+            decay_tiles[k] = decayed
 
-        def finish(c, i):
-            back = psum.tile([P, NEURONS], F32, tag="bank")
+        def turn_back(k):
+            c, i = divmod(k, ROW_TILES)
+            back = psum.tile([P, NEURONS], F32, tag="back", bufs=1, name="back")
             for j in range(BLOCKS):
                 nc.tensor.transpose(
-                    back[:, P * j : P * (j + 1)], update_tiles[(c, j)][:, P * i : P * (i + 1)], ident_f32[:]
+                    back[:, P * j : P * (j + 1)],
+                    update_tiles[BLOCKS * c + j][:, P * i : P * (i + 1)],
+                    ident_f32[:],
                 )
-            result = work.tile([P, NEURONS], F32, tag="result")
-            nc.vector.tensor_tensor(out=result[:], in0=back[:], in1=decay_tiles[(c, i)][:], op=ALU.add)
+            back_tiles[k] = back
+
+        def finish(k):
+            c, i = divmod(k, ROW_TILES)
+            result = work.tile([P, NEURONS], F32, tag="result", name="result")
+            nc.vector.tensor_tensor(
+                out=result[:].rearrange("p (m j) -> p m j", j=BLOCKS),
+                in0=back_tiles[k][:].rearrange("p (j m) -> p m j", j=BLOCKS),
+                in1=decay_tiles[k][:].rearrange("p (m j) -> p m j", j=BLOCKS),
+                op=ALU.add,
+            )
             nc.sync.dma_start(out=out_chunks[c][:, i, :], in_=result[:])
 
-        for g in range(PASSES):
-            turn_and_quantise(0, g)
-        nc.scalar.activation(out=a_rows[:], in_=tau_m_rows[:], func=ACT.Sigmoid)
-        for n in range(UNITS + FINISH_LAG):
-            c, q = divmod(n, STEPS)
-            if q == 0 and c + 2 < N_CHUNKS:
-                load_activations(c + 2)
-                load_state(c + 2)
-            if c + 1 < N_CHUNKS:
-                turn_and_quantise(c + 1, q)
-            if n < UNITS:
-                decay(c, q)
-                drive(c, q)
-                threshold(c, q)
-            if n >= FINISH_LAG:
-                finish(*divmod(n - FINISH_LAG, STEPS))
-            if n < UNITS:
-                reset_and_update(c, q)
+        def live(k):
+            return 0 <= k < UNITS
+
+        for n in range(-TURN_LEAD, UNITS + FINISH_LAG):
+            turning = n + TURN_LEAD
+            if live(turning):
+                c, q = divmod(turning, STEPS)
+                if q == 0 and 0 < c and c + 1 < N_CHUNKS:
+                    load_spk(c + 1)
+                    load_b(c + 1)
+                    load_x(c + 1)
+                    load_mem(c + 1)
+                turn(turning)
+                group(turning)
+            if live(n - FINISH_LAG):
+                turn_back(n - FINISH_LAG)
+            if live(turning) and turning % 2 == 1:
+                turn_b(turning // STEPS, turning % STEPS // 2)
+            if live(n + THRE_LEAD + 1):
+                spike_part(n + THRE_LEAD + 1)
+            if live(n + THRE_LEAD):
+                threshold(n + THRE_LEAD)
+            if n == -2:
+                permute_scales()
+                permute_words(0)
+                permute_words(1)
+            if n == -1:
+                permute_words(2)
+                permute_words(3)
+            if live(turning - 1):
+                quantise(turning - 1)
+            if live(n - FINISH_LAG):
+                finish(n - FINISH_LAG)
+            if live(n):
+                decay(n)
+                matmuls(n)
+            if live(n - 1):
+                update(n - 1)
+            if live(n + THRE_LEAD):
+                reset(n + THRE_LEAD)
+            if live(n + THRE_LEAD - 1):
+                offset(n + THRE_LEAD - 1)

@@ -311,7 +311,7 @@ def tile_snnlayer_pa_t_kernel(
         def decay(k):
             c, i = divmod(k, ROW_TILES)
             decayed = work.tile([P, NEURONS], F32, tag="decayed", bufs=8, name="decayed")
-            nc.gpsimd.tensor_tensor(out=decayed[:], in0=mem_tiles[c][:, i, :], in1=a_rows[:], op=ALU.mult)
+            nc.vector.tensor_tensor(out=decayed[:], in0=mem_tiles[c][:, i, :], in1=a_rows[:], op=ALU.mult)
             decay_tiles[k] = decayed
 
         def turn_back(k):

@@ -26,7 +26,8 @@ UNITS = N_CHUNKS * STEPS
 assert PASSES == STEPS and BLOCKS == STEPS and ROW_TILES == STEPS
 TURN_LEAD = STEPS
 THRE_LEAD = 2
-FINISH_LAG = STEPS + 1
+BACK_LAG = STEPS + 1
+FINISH_LAG = BACK_LAG + 1
 
 BASELINE_THRE = 0.1
 BETA = 1.8
@@ -75,20 +76,26 @@ def tile_snnlayer_pa_t_kernel(
         mem_tiles = {}
         b_tiles = {}
 
+        def load_rows(c, tile, rows):
+            pieces = 2 if c == 0 else 1
+            for piece in range(pieces):
+                part = slice(piece * ROW_TILES // pieces, (piece + 1) * ROW_TILES // pieces)
+                nc.sync.dma_start(out=tile[:, part, :], in_=rows[:, part, :])
+
         def load_spk(c):
             spk_tiles[c] = loads.tile([P, ROW_TILES, 2 * 512], BF16, tag="spk", name="spk_sb")
-            nc.sync.dma_start(out=spk_tiles[c][:], in_=spk_chunks[c])
+            load_rows(c, spk_tiles[c], spk_chunks[c])
 
         def load_x(c):
             x_tiles[c] = loads.tile([P, ROW_TILES, 2 * 512], BF16, tag="x", name="x_sb")
-            nc.sync.dma_start(out=x_tiles[c][:], in_=x_chunks[c])
+            load_rows(c, x_tiles[c], x_chunks[c])
 
         def load_b(c):
             b_tiles[c] = loads.tile([P, ROW_TILES, NEURONS], BF16, tag="b", name="b_sb")
             nc.sync.dma_start(out=b_tiles[c][:], in_=b_chunks[c])
 
         def load_mem(c):
-            mem_tiles[c] = loads.tile([P, ROW_TILES, NEURONS], BF16, tag="mem", name="mem_sb")
+            mem_tiles[c] = loads.tile([P, ROW_TILES, NEURONS], BF16, tag="mem", bufs=5, name="mem_sb")
             nc.sync.dma_start(out=mem_tiles[c][:], in_=mem_chunks[c])
 
         load_spk(0)
@@ -102,25 +109,28 @@ def tile_snnlayer_pa_t_kernel(
             nc.scalar.dma_start(out=vec_rows[v : v + 1, :], in_=vector.rearrange("(o n) -> o n", o=1))
 
         w_words = const.tile([P, PASSES, NEURONS], I32, align_bytes=64)
-        w_planes = const.tile([P, PASSES, NEURONS], U8, align_bytes=64)
-        nc.vector.memset(w_planes[:].rearrange("p g n -> p (g n)").bitcast(I32), 0)
+        w_planes = const.tile([P, NEURONS], U8, align_bytes=64)
+        nc.vector.memset(w_planes[:].bitcast(I32), 0)
         for quadrant in range(4):
             rows = slice(4 * quadrant, 4 * quadrant + 4)
-            live = slice(32 * quadrant, 32 * quadrant + 4)
-            nc.sync.dma_start(out=w_planes[live, 0, :].bitcast(I32), in_=W_rec4in_scales[0, rows, :].bitcast(I32))
-            nc.sync.dma_start(out=w_planes[live, 1, :].bitcast(I32), in_=W_out2in_scales[0, rows, :].bitcast(I32))
+            first = 32 * quadrant
+            nc.sync.dma_start(out=w_planes[first : first + 4, :].bitcast(I32), in_=W_rec4in_scales[0, rows, :].bitcast(I32))
             nc.sync.dma_start(
-                out=w_planes[live, 2:4, :].bitcast(I32),
-                in_=W_x2in_scales[:, rows, :].rearrange("g r n -> r g n").bitcast(I32),
+                out=w_planes[first + 4 : first + 8, :].bitcast(I32), in_=W_out2in_scales[0, rows, :].bitcast(I32)
             )
+            for g in (0, 1):
+                nc.sync.dma_start(
+                    out=w_planes[first + 8 + 4 * g : first + 12 + 4 * g, :].bitcast(I32),
+                    in_=W_x2in_scales[g, rows, :].bitcast(I32),
+                )
         nc.sync.dma_start(out=w_words[:, 0, :], in_=W_rec4in_words[0].rearrange("p n t -> p (n t)").bitcast(I32))
         nc.sync.dma_start(out=w_words[:, 1, :], in_=W_out2in_words[0].rearrange("p n t -> p (n t)").bitcast(I32))
         nc.sync.dma_start(
             out=w_words[:, 2:4, :], in_=W_x2in_words.rearrange("g p n t -> p g (n t)").bitcast(I32)
         )
-        load_mem(0)
         load_spk(1)
         load_b(1)
+        load_mem(0)
         load_x(1)
         load_mem(1)
 
@@ -167,13 +177,16 @@ def tile_snnlayer_pa_t_kernel(
             out=thre_spk[:], in0=p_col[:], scalar1=-BETA, scalar2=BETA, op0=ALU.mult, op1=ALU.add
         )
 
+        baseline = const.tile([P, 1], F32)
+        nc.vector.memset(baseline[:], BASELINE_THRE)
+
         w_codes = const.tile([P, PASSES, NEURONS], I32, align_bytes=64)
-        w_scales = const.tile([P, PASSES, NEURONS], U8, align_bytes=64)
+        w_scales = const.tile([P, NEURONS], U8, align_bytes=64)
 
         def permute_scales():
             nc.vector.tensor_copy(
-                out=w_scales[:].rearrange("p g (j m) -> p g m j", j=BLOCKS),
-                in_=w_planes[:].rearrange("p g (m j) -> p g m j", j=BLOCKS),
+                out=w_scales[:].rearrange("p (j m) -> p m j", j=BLOCKS),
+                in_=w_planes[:].rearrange("p (m j) -> p m j", j=BLOCKS),
             )
 
         def permute_words(g):
@@ -237,17 +250,23 @@ def tile_snnlayer_pa_t_kernel(
             c, j = divmod(k, BLOCKS)
             return grouped_tiles[PASSES * c][:].rearrange("p (s t) -> p t s", t=4)[:, j, :]
 
-        def turn_b(c, u):
-            turned = psum.tile([P, CHUNK], F32, tag="b_turned", name="b_turned")
+        def turn_b(k):
+            c, q = divmod(k, STEPS)
+            u, half = divmod(q, 2)
+            if half == 0:
+                b_turned_tiles[(c, u)] = psum.tile([P, CHUNK], F32, tag="b_turned", name="b_turned")
             source = b_tiles[c][:].bitcast(F32)
-            for i in range(ROW_TILES):
-                nc.tensor.transpose(turned[:, P * i : P * (i + 1)], source[:, i, u:WORDS:2], ident_f32[:])
-            b_turned_tiles[(c, u)] = turned
+            for i in (2 * half, 2 * half + 1):
+                nc.tensor.transpose(
+                    b_turned_tiles[(c, u)][:, P * i : P * (i + 1)], source[:, i, u:WORDS:2], ident_f32[:]
+                )
 
         def spike_part(k):
             j = k % BLOCKS
             part = work.tile([P, CHUNK], F32, tag="spk_part", name="spk_part")
-            nc.scalar.activation(out=part[:], in_=spikes(k), func=ACT.Identity, scale=thre_spk[:, j : j + 1])
+            nc.scalar.activation(
+                out=part[:], in_=spikes(k), func=ACT.Identity, scale=thre_spk[:, j : j + 1], bias=baseline[:]
+            )
             spk_part_tiles[k] = part
 
         def threshold(k):
@@ -266,9 +285,7 @@ def tile_snnlayer_pa_t_kernel(
 
         def reset(k):
             product = work.tile([P, CHUNK], F32, tag="reset", name="reset")
-            nc.vector.scalar_tensor_tensor(
-                out=product[:], in0=thre_tiles[k][:], scalar=BASELINE_THRE, in1=spikes(k), op0=ALU.add, op1=ALU.mult
-            )
+            nc.gpsimd.tensor_tensor(out=product[:], in0=thre_tiles[k][:], in1=spikes(k), op=ALU.mult)
             reset_tiles[k] = product
 
         def offset(k):
@@ -287,7 +304,7 @@ def tile_snnlayer_pa_t_kernel(
                 nc.tensor.matmul_mx(
                     out=sums[:],
                     lhsT=w_codes[:, g, neurons].bitcast(FP8X4),
-                    lhsT_scale=w_scales[:, g, neurons],
+                    lhsT_scale=w_scales[4 * g : P, neurons],
                     rhs=codes_tiles[c][:, g, :].bitcast(FP8X4),
                     rhs_scale=planes_tiles[c][:, g, :],
                     start=(g == 0),
@@ -310,13 +327,16 @@ def tile_snnlayer_pa_t_kernel(
 
         def decay(k):
             c, i = divmod(k, ROW_TILES)
-            decayed = work.tile([P, NEURONS], F32, tag="decayed", bufs=8, name="decayed")
+            decayed = work.tile([P, NEURONS], F32, tag="decayed", name="decayed")
             nc.vector.tensor_tensor(out=decayed[:], in0=mem_tiles[c][:, i, :], in1=a_rows[:], op=ALU.mult)
             decay_tiles[k] = decayed
 
         def turn_back(k):
             c, i = divmod(k, ROW_TILES)
-            back = psum.tile([P, NEURONS], F32, tag="back", bufs=1, name="back")
+            if k + BACK_LAG < UNITS:
+                back = psum.tile([P, NEURONS], F32, tag="back", bufs=1, name="back")
+            else:
+                back = psum.tile([P, NEURONS], F32, tag="turned", bufs=3, name="back_last")
             for j in range(BLOCKS):
                 nc.tensor.transpose(
                     back[:, P * j : P * (j + 1)],
@@ -341,40 +361,36 @@ def tile_snnlayer_pa_t_kernel(
 
         for n in range(-TURN_LEAD, UNITS + FINISH_LAG):
             turning = n + TURN_LEAD
-            if live(turning):
-                c, q = divmod(turning, STEPS)
-                if q == 0 and 0 < c and c + 1 < N_CHUNKS:
-                    load_spk(c + 1)
-                    load_b(c + 1)
-                    load_x(c + 1)
-                    load_mem(c + 1)
-                turn(turning)
-                group(turning)
-            if live(n - FINISH_LAG):
-                turn_back(n - FINISH_LAG)
-            if live(turning) and turning % 2 == 1:
-                turn_b(turning // STEPS, turning % STEPS // 2)
-            if live(n + THRE_LEAD + 1):
-                spike_part(n + THRE_LEAD + 1)
-            if live(n + THRE_LEAD):
-                threshold(n + THRE_LEAD)
-            if n == -2:
-                permute_scales()
-                permute_words(0)
-                permute_words(1)
-            if n == -1:
-                permute_words(2)
-                permute_words(3)
+            if live(turning) and turning % STEPS == 0 and 0 < turning // STEPS < N_CHUNKS - 1:
+                load_spk(turning // STEPS + 1)
+                load_b(turning // STEPS + 1)
+                load_x(turning // STEPS + 1)
+                load_mem(turning // STEPS + 1)
             if live(turning - 1):
                 quantise(turning - 1)
+            if live(n + THRE_LEAD):
+                threshold(n + THRE_LEAD)
+                reset(n + THRE_LEAD)
             if live(n - FINISH_LAG):
                 finish(n - FINISH_LAG)
-            if live(n):
-                decay(n)
-                matmuls(n)
             if live(n - 1):
                 update(n - 1)
-            if live(n + THRE_LEAD):
-                reset(n + THRE_LEAD)
+            if live(n - FINISH_LAG + 2):
+                decay(n - FINISH_LAG + 2)
+            if live(n):
+                matmuls(n)
             if live(n + THRE_LEAD - 1):
                 offset(n + THRE_LEAD - 1)
+            if live(n + THRE_LEAD + 1):
+                spike_part(n + THRE_LEAD + 1)
+            if live(turning):
+                turn(turning)
+                group(turning)
+            if live(n - BACK_LAG):
+                turn_back(n - BACK_LAG)
+            if live(turning):
+                turn_b(turning)
+            if n == -1:
+                permute_scales()
+                for g in range(PASSES):
+                    permute_words(g)

@@ -24,10 +24,10 @@ WORDS = 256
 STEPS = 4
 UNITS = N_CHUNKS * STEPS
 assert PASSES == STEPS and BLOCKS == STEPS and ROW_TILES == STEPS
-TURN_LEAD = STEPS
-THRE_LEAD = 2
+TURN_LEAD = STEPS + 1
 BACK_LAG = STEPS + 1
 FINISH_LAG = BACK_LAG + 1
+SPREAD_FROM = 6
 
 BASELINE_THRE = 0.1
 BETA = 1.8
@@ -136,49 +136,20 @@ def tile_snnlayer_pa_t_kernel(
 
         ident_f32 = const.tile([P, P], F32)
         make_identity(nc, ident_f32[:])
-        ident_bf16 = const.tile([P, P], BF16)
-        make_identity(nc, ident_bf16[:])
 
-        vec_ps = psum.tile([P, 2, P], F32, tag="turned", bufs=3)
-        vec_words = vec_rows[:].bitcast(F32)
-        for u in (0, 1):
-            nc.tensor.transpose(vec_ps[:, u, :], vec_words[:, u:WORDS:2], ident_f32[:])
-        tau_ps = psum.tile([P, NEURONS], F32, tag="sums")
-        nc.tensor.matmul(
-            tau_ps[:], lhsT=ident_bf16[:, 4:5].to_broadcast([P, P]), rhs=vec_rows[:], start=True, stop=True
-        )
         vec_cols = const.tile([P, len(vectors), BLOCKS], F32)
-        for u in (0, 1):
-            nc.vector.tensor_copy(
-                out=vec_cols[:, :, 2 * u : 2 * u + 2],
-                in_=vec_ps[:, u, :].bitcast(BF16).rearrange("p (v e) -> p v e", e=2)[:, 0 : len(vectors), :],
-            )
         p_col = const.tile([P, BLOCKS], F32)
         a_col = const.tile([P, BLOCKS], F32)
-        nc.scalar.activation(out=p_col[:], in_=vec_cols[:, 3, :], func=ACT.Sigmoid)
-        nc.scalar.activation(out=a_col[:], in_=vec_cols[:, 4, :], func=ACT.Sigmoid)
-        a_rows = const.tile([P, NEURONS], F32)
-        nc.scalar.activation(out=a_rows[:], in_=tau_ps[:], func=ACT.Sigmoid)
-
         bias_two = const.tile([P, BLOCKS], F32)
         bias_sum = const.tile([P, BLOCKS], F32)
-        nc.vector.tensor_tensor(out=bias_two[:], in0=vec_cols[:, 0, :], in1=vec_cols[:, 1, :], op=ALU.add)
-        nc.vector.tensor_tensor(out=bias_sum[:], in0=bias_two[:], in1=vec_cols[:, 2, :], op=ALU.add)
         drive_gain = const.tile([P, BLOCKS], F32)
         drive_bias = const.tile([P, BLOCKS], F32)
-        nc.vector.tensor_scalar(
-            out=drive_gain[:], in0=a_col[:], scalar1=-R_M, scalar2=R_M, op0=ALU.mult, op1=ALU.add
-        )
-        nc.vector.tensor_tensor(out=drive_bias[:], in0=drive_gain[:], in1=bias_sum[:], op=ALU.mult)
         thre_b = const.tile([P, BLOCKS], F32)
         thre_spk = const.tile([P, BLOCKS], F32)
-        nc.vector.tensor_scalar(out=thre_b[:], in0=p_col[:], scalar1=BETA, scalar2=None, op0=ALU.mult)
-        nc.vector.tensor_scalar(
-            out=thre_spk[:], in0=p_col[:], scalar1=-BETA, scalar2=BETA, op0=ALU.mult, op1=ALU.add
-        )
-
         baseline = const.tile([P, 1], F32)
         nc.vector.memset(baseline[:], BASELINE_THRE)
+        a_rows = psum.tile([P, NEURONS], F32, tag="a_rows", bufs=1)
+        a_rows_sb = const.tile([P, NEURONS], F32)
 
         w_codes = const.tile([P, PASSES, NEURONS], I32, align_bytes=64)
         w_scales = const.tile([P, NEURONS], U8, align_bytes=64)
@@ -195,7 +166,38 @@ def tile_snnlayer_pa_t_kernel(
                 in_=w_words[:, g, :].rearrange("p (m j) -> p j m", j=BLOCKS),
             )
 
+        def constants():
+            vec_ps = psum.tile([P, 2, P], F32, tag="turned", bufs=2, name="vec_ps")
+            vec_words = vec_rows[:].bitcast(F32)
+            for u in (0, 1):
+                nc.tensor.transpose(vec_ps[:, u, :], vec_words[:, u:WORDS:2], ident_f32[:])
+            for u in (0, 1):
+                nc.vector.tensor_copy(
+                    out=vec_cols[:, :, 2 * u : 2 * u + 2],
+                    in_=vec_ps[:, u, :].bitcast(BF16).rearrange("p (v e) -> p v e", e=2)[:, 0 : len(vectors), :],
+                )
+            nc.scalar.activation(out=p_col[:], in_=vec_cols[:, 3, :], func=ACT.Sigmoid)
+            nc.scalar.activation(out=a_col[:], in_=vec_cols[:, 4, :], func=ACT.Sigmoid)
+            nc.vector.tensor_scalar(
+                out=thre_spk[:], in0=p_col[:], scalar1=-BETA, scalar2=BETA, op0=ALU.mult, op1=ALU.add
+            )
+            nc.vector.tensor_scalar(out=thre_b[:], in0=p_col[:], scalar1=BETA, scalar2=None, op0=ALU.mult)
+            nc.vector.tensor_tensor(out=bias_two[:], in0=vec_cols[:, 0, :], in1=vec_cols[:, 1, :], op=ALU.add)
+            nc.vector.tensor_scalar(
+                out=drive_gain[:], in0=a_col[:], scalar1=-R_M, scalar2=R_M, op0=ALU.mult, op1=ALU.add
+            )
+            nc.vector.tensor_tensor(out=bias_sum[:], in0=bias_two[:], in1=vec_cols[:, 2, :], op=ALU.add)
+            nc.vector.tensor_tensor(out=drive_bias[:], in0=drive_gain[:], in1=bias_sum[:], op=ALU.mult)
+
+        def decay_rows():
+            for j in range(BLOCKS):
+                nc.tensor.transpose(
+                    a_rows[:, P * j : P * (j + 1)], a_col[:, j : j + 1].to_broadcast([P, P]), ident_f32[:]
+                )
+            nc.scalar.copy(out=a_rows_sb[:], in_=a_rows[:])
+
         turned_tiles = {}
+        spread_tiles = {}
         grouped_tiles = {}
         codes_tiles = {}
         planes_tiles = {}
@@ -209,33 +211,51 @@ def tile_snnlayer_pa_t_kernel(
         decay_tiles = {}
         back_tiles = {}
 
-        def turn(k):
+        def turn_half(k, bank):
             c, g = divmod(k, PASSES)
             source = (spk_tiles[c] if g < 2 else x_tiles[c])[:].bitcast(F32)
             first_word = (WORDS, 0, 0, WORDS)[g]
-            for bank in range(ROW_TILES // 2):
-                turned = psum.tile([P, 2, 2 * P], F32, tag="turned", bufs=3, name="turned")
-                for i in (0, 1):
-                    for u in (0, 1):
-                        nc.tensor.transpose(
-                            turned[:, u, P * i : P * (i + 1)],
-                            source[:, 2 * bank + i, first_word + u : first_word + WORDS : 2],
-                            ident_f32[:],
-                        )
-                turned_tiles[(k, bank)] = turned
+            if k < PASSES and bank == 1:
+                turned = psum.tile([P, 2, 2 * P], F32, tag="sums", name="turned_first")
+            else:
+                turned = psum.tile([P, 2, 2 * P], F32, tag="turned", bufs=2, name="turned")
+            for i in (0, 1):
+                for u in (0, 1):
+                    if bank == 1 and k in spread_tiles:
+                        words = spread_tiles[k][:, i, u, :]
+                    else:
+                        words = source[:, 2 * bank + i, first_word + u : first_word + WORDS : 2]
+                    nc.tensor.transpose(turned[:, u, P * i : P * (i + 1)], words, ident_f32[:])
+            turned_tiles[k] = turned
 
-        def group(k):
-            spike = k % PASSES == 0
-            grouped = quant.tile(
-                [P, 4 * CHUNK], BF16, tag="grouped_in" if spike else "grouped", bufs=3, name="grouped", align_bytes=64
+        def spread(k):
+            if k < SPREAD_FROM:
+                return
+            c, g = divmod(k, PASSES)
+            source = (spk_tiles[c] if g < 2 else x_tiles[c])[:].bitcast(F32)
+            first_word = (WORDS, 0, 0, WORDS)[g]
+            spread_tiles[k] = quant.tile([P, 2, 2, P], F32, tag="spread", bufs=3, name="spread_words")
+            nc.scalar.copy(
+                out=spread_tiles[k][:],
+                in_=source[:, 2:4, first_word : first_word + WORDS].rearrange("p i (w u) -> p i u w", u=2),
             )
-            words = grouped[:].bitcast(F32).rearrange("p (s u) -> p s u", u=2)
-            for bank in range(ROW_TILES // 2):
-                nc.scalar.copy(
-                    out=words[:, 2 * P * bank : 2 * P * (bank + 1), :],
-                    in_=turned_tiles[(k, bank)][:].rearrange("p u s -> p s u"),
+
+        def group_half(k, bank):
+            if bank == 0:
+                spike = k % PASSES == 0
+                grouped_tiles[k] = quant.tile(
+                    [P, 4 * CHUNK],
+                    BF16,
+                    tag="grouped_in" if spike else "grouped",
+                    bufs=3,
+                    name="grouped",
+                    align_bytes=64,
                 )
-            grouped_tiles[k] = grouped
+            words = grouped_tiles[k][:].bitcast(F32).rearrange("p (s u) -> p s u", u=2)
+            copy = nc.vector.tensor_copy if k < PASSES and bank == 1 else nc.scalar.copy
+            copy(
+                out=words[:, 2 * P * bank : 2 * P * (bank + 1), :], in_=turned_tiles[k][:].rearrange("p u s -> p s u")
+            )
 
         def quantise(k):
             c, g = divmod(k, PASSES)
@@ -299,10 +319,10 @@ def tile_snnlayer_pa_t_kernel(
         def matmuls(k):
             c, j = divmod(k, BLOCKS)
             neurons = slice(P * j, P * (j + 1))
-            sums = psum.tile([P, CHUNK], F32, tag="sums", name="sums")
+            sums_tiles[k] = psum.tile([P, CHUNK], F32, tag="sums", name="sums")
             for g in range(PASSES):
                 nc.tensor.matmul_mx(
-                    out=sums[:],
+                    out=sums_tiles[k][:],
                     lhsT=w_codes[:, g, neurons].bitcast(FP8X4),
                     lhsT_scale=w_scales[4 * g : P, neurons],
                     rhs=codes_tiles[c][:, g, :].bitcast(FP8X4),
@@ -310,7 +330,6 @@ def tile_snnlayer_pa_t_kernel(
                     start=(g == 0),
                     stop=(g == PASSES - 1),
                 )
-            sums_tiles[k] = sums
 
         def update(k):
             j = k % BLOCKS
@@ -327,16 +346,24 @@ def tile_snnlayer_pa_t_kernel(
 
         def decay(k):
             c, i = divmod(k, ROW_TILES)
-            decayed = work.tile([P, NEURONS], F32, tag="decayed", name="decayed")
-            nc.vector.tensor_tensor(out=decayed[:], in0=mem_tiles[c][:, i, :], in1=a_rows[:], op=ALU.mult)
+            decayed = work.tile([P, NEURONS], F32, tag="decayed", bufs=8, name="decayed")
+            engine = nc.gpsimd if (k >= UNITS - ROW_TILES) else nc.vector
+            engine.tensor_tensor(
+                out=decayed[:].rearrange("p (m j) -> p m j", j=BLOCKS),
+                in0=mem_tiles[c][:, i, :].rearrange("p (m j) -> p m j", j=BLOCKS),
+                in1=(a_rows_sb if (k >= UNITS - ROW_TILES) else a_rows)[:].rearrange("p (j m) -> p m j", j=BLOCKS),
+                op=ALU.mult,
+            )
             decay_tiles[k] = decayed
 
         def turn_back(k):
             c, i = divmod(k, ROW_TILES)
-            if k + BACK_LAG < UNITS:
+            if k < UNITS - ROW_TILES:
                 back = psum.tile([P, NEURONS], F32, tag="back", bufs=1, name="back")
+            elif k % 2 == 0:
+                back = psum.tile([P, NEURONS], F32, tag="turned", bufs=2, name="back_last")
             else:
-                back = psum.tile([P, NEURONS], F32, tag="turned", bufs=3, name="back_last")
+                back = psum.tile([P, NEURONS], F32, tag="b_turned", name="back_last")
             for j in range(BLOCKS):
                 nc.tensor.transpose(
                     back[:, P * j : P * (j + 1)],
@@ -347,7 +374,7 @@ def tile_snnlayer_pa_t_kernel(
 
         def finish(k):
             c, i = divmod(k, ROW_TILES)
-            result = work.tile([P, NEURONS], F32, tag="result", name="result")
+            result = work.tile([P, NEURONS], F32, tag="result", bufs=8, name="result")
             nc.vector.tensor_tensor(
                 out=result[:].rearrange("p (m j) -> p m j", j=BLOCKS),
                 in0=back_tiles[k][:].rearrange("p (j m) -> p m j", j=BLOCKS),
@@ -356,41 +383,42 @@ def tile_snnlayer_pa_t_kernel(
             )
             nc.sync.dma_start(out=out_chunks[c][:, i, :], in_=result[:])
 
+        def turn(k):
+            for bank in range(ROW_TILES // 2):
+                turn_half(k, bank)
+                group_half(k, bank)
+
         def live(k):
             return 0 <= k < UNITS
 
+        def load(k):
+            c, q = divmod(k, STEPS)
+            if q == 0 and 0 < c < N_CHUNKS - 1:
+                load_spk(c + 1)
+                load_b(c + 1)
+                load_x(c + 1)
+                load_mem(c + 1)
+
+        def turn_late(k):
+            if k == STEPS:
+                return
+            if k == STEPS + 1:
+                turn(STEPS)
+            turn(k)
+
+        step = ((load, 4), (quantise, 3), (threshold, 2), (reset, 2), (finish, -6), (update, -1), (decay, 0), (matmuls, 0), (offset, 1), (spike_part, 3), (turn_late, 5), (turn_back, -5), (turn_b, 4), (spread, 6))
         for n in range(-TURN_LEAD, UNITS + FINISH_LAG):
-            turning = n + TURN_LEAD
-            if live(turning) and turning % STEPS == 0 and 0 < turning // STEPS < N_CHUNKS - 1:
-                load_spk(turning // STEPS + 1)
-                load_b(turning // STEPS + 1)
-                load_x(turning // STEPS + 1)
-                load_mem(turning // STEPS + 1)
-            if live(turning - 1):
-                quantise(turning - 1)
-            if live(n + THRE_LEAD):
-                threshold(n + THRE_LEAD)
-                reset(n + THRE_LEAD)
-            if live(n - FINISH_LAG):
-                finish(n - FINISH_LAG)
-            if live(n - 1):
-                update(n - 1)
-            if live(n - FINISH_LAG + 2):
-                decay(n - FINISH_LAG + 2)
-            if live(n):
-                matmuls(n)
-            if live(n + THRE_LEAD - 1):
-                offset(n + THRE_LEAD - 1)
-            if live(n + THRE_LEAD + 1):
-                spike_part(n + THRE_LEAD + 1)
-            if live(turning):
-                turn(turning)
-                group(turning)
-            if live(n - BACK_LAG):
-                turn_back(n - BACK_LAG)
-            if live(turning):
-                turn_b(turning)
-            if n == -1:
+            if n == -2:
                 permute_scales()
-                for g in range(PASSES):
-                    permute_words(g)
+                permute_words(0)
+                permute_words(1)
+            if n == -2 + 1:
+                permute_words(2)
+                permute_words(3)
+            for stage, offset_in_units in step:
+                if live(n + offset_in_units):
+                    stage(n + offset_in_units)
+            if n == -TURN_LEAD:
+                constants()
+            if n == -TURN_LEAD + 2:
+                decay_rows()

@@ -27,7 +27,7 @@ assert PASSES == STEPS and BLOCKS == STEPS and ROW_TILES == STEPS
 TURN_LEAD = STEPS + 1
 BACK_LAG = STEPS + 1
 FINISH_LAG = BACK_LAG + 1
-SPREAD_FROM = 6
+SPREAD_FROM = 8
 
 BASELINE_THRE = 0.1
 BETA = 1.8
@@ -77,7 +77,7 @@ def tile_snnlayer_pa_t_kernel(
         b_tiles = {}
 
         def load_rows(c, tile, rows):
-            pieces = 2 if c == 0 else 1
+            pieces = 1 if c == 0 else 1
             for piece in range(pieces):
                 part = slice(piece * ROW_TILES // pieces, (piece + 1) * ROW_TILES // pieces)
                 nc.sync.dma_start(out=tile[:, part, :], in_=rows[:, part, :])
@@ -88,7 +88,7 @@ def tile_snnlayer_pa_t_kernel(
 
         def load_x(c):
             x_tiles[c] = loads.tile([P, ROW_TILES, 2 * 512], BF16, tag="x", name="x_sb")
-            load_rows(c, x_tiles[c], x_chunks[c])
+            nc.sync.dma_start(out=x_tiles[c][:], in_=x_chunks[c])
 
         def load_b(c):
             b_tiles[c] = loads.tile([P, ROW_TILES, NEURONS], BF16, tag="b", name="b_sb")
@@ -98,44 +98,54 @@ def tile_snnlayer_pa_t_kernel(
             mem_tiles[c] = loads.tile([P, ROW_TILES, NEURONS], BF16, tag="mem", bufs=5, name="mem_sb")
             nc.sync.dma_start(out=mem_tiles[c][:], in_=mem_chunks[c])
 
-        load_spk(0)
-        load_b(0)
-        load_x(0)
-
         vectors = [b_x2in, b_rec4in, b_out2in, tau_adp_in, tau_m_in]
         vec_rows = const.tile([P, NEURONS], BF16)
         nc.vector.memset(vec_rows[:], 0.0)
-        for v, vector in enumerate(vectors):
-            nc.scalar.dma_start(out=vec_rows[v : v + 1, :], in_=vector.rearrange("(o n) -> o n", o=1))
 
         w_words = const.tile([P, PASSES, NEURONS], I32, align_bytes=64)
-        w_planes = const.tile([P, NEURONS], U8, align_bytes=64)
-        nc.vector.memset(w_planes[:].bitcast(I32), 0)
-        for quadrant in range(4):
-            rows = slice(4 * quadrant, 4 * quadrant + 4)
-            first = 32 * quadrant
-            nc.sync.dma_start(out=w_planes[first : first + 4, :].bitcast(I32), in_=W_rec4in_scales[0, rows, :].bitcast(I32))
-            nc.sync.dma_start(
-                out=w_planes[first + 4 : first + 8, :].bitcast(I32), in_=W_out2in_scales[0, rows, :].bitcast(I32)
-            )
-            for g in (0, 1):
+        w_planes = const.tile([P, 2, NEURONS], U8, align_bytes=64)
+        nc.vector.memset(w_planes[:].rearrange("p h n -> p (h n)").bitcast(I32), 0)
+
+        def load_scales(g, quadrants):
+            source = (W_rec4in_scales[0], W_out2in_scales[0], W_x2in_scales[0], W_x2in_scales[1])[g]
+            for quadrant in quadrants:
+                first = 32 * quadrant + 4 * (g % 2)
                 nc.sync.dma_start(
-                    out=w_planes[first + 8 + 4 * g : first + 12 + 4 * g, :].bitcast(I32),
-                    in_=W_x2in_scales[g, rows, :].bitcast(I32),
+                    out=w_planes[first : first + 4, g // 2, :].bitcast(I32),
+                    in_=source[4 * quadrant : 4 * quadrant + 4, :].bitcast(I32),
                 )
-        nc.sync.dma_start(out=w_words[:, 0, :], in_=W_rec4in_words[0].rearrange("p n t -> p (n t)").bitcast(I32))
-        nc.sync.dma_start(out=w_words[:, 1, :], in_=W_out2in_words[0].rearrange("p n t -> p (n t)").bitcast(I32))
-        nc.sync.dma_start(
-            out=w_words[:, 2:4, :], in_=W_x2in_words.rearrange("g p n t -> p g (n t)").bitcast(I32)
-        )
+
+        def load_words(g):
+            if g < 2:
+                source = (W_rec4in_words, W_out2in_words)[g]
+                nc.sync.dma_start(out=w_words[:, g, :], in_=source[0].rearrange("p n t -> p (n t)").bitcast(I32))
+            else:
+                nc.sync.dma_start(
+                    out=w_words[:, 2:4, :], in_=W_x2in_words.rearrange("g p n t -> p g (n t)").bitcast(I32)
+                )
+
+        def load_vectors():
+            for v, vector in enumerate(vectors):
+                nc.scalar.dma_start(out=vec_rows[v : v + 1, :], in_=vector.rearrange("(o n) -> o n", o=1))
+
+        ident_f32 = const.tile([P, P], F32)
+        make_identity(nc, ident_f32[:])
+        load_scales(0, range(4))
+        load_spk(0)
+        load_vectors()
+        load_b(0)
+        load_x(0)
+        load_words(0)
+        load_scales(1, range(4))
+        load_words(1)
+        load_words(2)
+        load_scales(2, range(4))
         load_spk(1)
+        load_scales(3, range(4))
         load_b(1)
         load_mem(0)
         load_x(1)
         load_mem(1)
-
-        ident_f32 = const.tile([P, P], F32)
-        make_identity(nc, ident_f32[:])
 
         vec_cols = const.tile([P, len(vectors), BLOCKS], F32)
         p_col = const.tile([P, BLOCKS], F32)
@@ -152,12 +162,12 @@ def tile_snnlayer_pa_t_kernel(
         a_rows_sb = const.tile([P, NEURONS], F32)
 
         w_codes = const.tile([P, PASSES, NEURONS], I32, align_bytes=64)
-        w_scales = const.tile([P, NEURONS], U8, align_bytes=64)
+        w_scales = const.tile([P, 2, NEURONS], U8, align_bytes=64)
 
-        def permute_scales():
+        def permute_scales(half):
             nc.vector.tensor_copy(
-                out=w_scales[:].rearrange("p (j m) -> p m j", j=BLOCKS),
-                in_=w_planes[:].rearrange("p (m j) -> p m j", j=BLOCKS),
+                out=w_scales[:, half, :].rearrange("p (j m) -> p m j", j=BLOCKS),
+                in_=w_planes[:, half, :].rearrange("p (m j) -> p m j", j=BLOCKS),
             )
 
         def permute_words(g):
@@ -252,7 +262,7 @@ def tile_snnlayer_pa_t_kernel(
                     align_bytes=64,
                 )
             words = grouped_tiles[k][:].bitcast(F32).rearrange("p (s u) -> p s u", u=2)
-            copy = nc.vector.tensor_copy if k < PASSES and bank == 1 else nc.scalar.copy
+            copy = nc.vector.tensor_copy if k < 2 and bank == 1 else nc.scalar.copy
             copy(
                 out=words[:, 2 * P * bank : 2 * P * (bank + 1), :], in_=turned_tiles[k][:].rearrange("p u s -> p s u")
             )
@@ -324,7 +334,7 @@ def tile_snnlayer_pa_t_kernel(
                 nc.tensor.matmul_mx(
                     out=sums_tiles[k][:],
                     lhsT=w_codes[:, g, neurons].bitcast(FP8X4),
-                    lhsT_scale=w_scales[4 * g : P, neurons],
+                    lhsT_scale=w_scales[4 * (g % 2) : P, g // 2, neurons],
                     rhs=codes_tiles[c][:, g, :].bitcast(FP8X4),
                     rhs_scale=planes_tiles[c][:, g, :],
                     start=(g == 0),
@@ -346,19 +356,32 @@ def tile_snnlayer_pa_t_kernel(
 
         def decay(k):
             c, i = divmod(k, ROW_TILES)
-            decayed = work.tile([P, NEURONS], F32, tag="decayed", bufs=8, name="decayed")
-            engine = nc.gpsimd if (k >= UNITS - ROW_TILES) else nc.vector
-            engine.tensor_tensor(
-                out=decayed[:].rearrange("p (m j) -> p m j", j=BLOCKS),
-                in0=mem_tiles[c][:, i, :].rearrange("p (m j) -> p m j", j=BLOCKS),
-                in1=(a_rows_sb if (k >= UNITS - ROW_TILES) else a_rows)[:].rearrange("p (j m) -> p m j", j=BLOCKS),
+            decay_tiles[k] = work.tile([P, NEURONS], F32, tag="decayed", bufs=8, name="decayed")
+            cols = 0 if k >= UNITS - ROW_TILES else NEURONS
+            if cols == 0:
+                return
+            nc.vector.tensor_tensor(
+                out=decay_tiles[k][:, 0:cols].rearrange("p (m j) -> p m j", j=BLOCKS),
+                in0=mem_tiles[c][:, i, 0:cols].rearrange("p (m j) -> p m j", j=BLOCKS),
+                in1=a_rows[:].rearrange("p (j m) -> p m j", j=BLOCKS)[:, 0 : cols // BLOCKS, :],
                 op=ALU.mult,
             )
-            decay_tiles[k] = decayed
+
+        def decay_rest(k):
+            c, i = divmod(k, ROW_TILES)
+            cols = 0 if k >= UNITS - ROW_TILES else NEURONS
+            if cols == NEURONS:
+                return
+            nc.gpsimd.tensor_tensor(
+                out=decay_tiles[k][:, cols:].rearrange("p (m j) -> p m j", j=BLOCKS),
+                in0=mem_tiles[c][:, i, cols:].rearrange("p (m j) -> p m j", j=BLOCKS),
+                in1=a_rows_sb[:].rearrange("p (j m) -> p m j", j=BLOCKS)[:, cols // BLOCKS :, :],
+                op=ALU.mult,
+            )
 
         def turn_back(k):
             c, i = divmod(k, ROW_TILES)
-            if k < UNITS - ROW_TILES:
+            if k < UNITS - 2 * ROW_TILES or (k < UNITS - ROW_TILES and k % 2 == 1):
                 back = psum.tile([P, NEURONS], F32, tag="back", bufs=1, name="back")
             elif k % 2 == 0:
                 back = psum.tile([P, NEURONS], F32, tag="turned", bufs=2, name="back_last")
@@ -375,13 +398,17 @@ def tile_snnlayer_pa_t_kernel(
         def finish(k):
             c, i = divmod(k, ROW_TILES)
             result = work.tile([P, NEURONS], F32, tag="result", bufs=8, name="result")
-            nc.vector.tensor_tensor(
-                out=result[:].rearrange("p (m j) -> p m j", j=BLOCKS),
-                in0=back_tiles[k][:].rearrange("p (j m) -> p m j", j=BLOCKS),
-                in1=decay_tiles[k][:].rearrange("p (m j) -> p m j", j=BLOCKS),
-                op=ALU.add,
-            )
-            nc.sync.dma_start(out=out_chunks[c][:, i, :], in_=result[:])
+            pieces = 2 if k == UNITS - 1 else 1
+            for piece in range(pieces):
+                cols = slice(piece * P // pieces, (piece + 1) * P // pieces)
+                ncols = slice(piece * NEURONS // pieces, (piece + 1) * NEURONS // pieces)
+                nc.vector.tensor_tensor(
+                    out=result[:].rearrange("p (m j) -> p m j", j=BLOCKS)[:, cols, :],
+                    in0=back_tiles[k][:].rearrange("p (j m) -> p m j", j=BLOCKS)[:, cols, :],
+                    in1=decay_tiles[k][:].rearrange("p (m j) -> p m j", j=BLOCKS)[:, cols, :],
+                    op=ALU.add,
+                )
+                nc.sync.dma_start(out=out_chunks[c][:, i, ncols], in_=result[:, ncols])
 
         def turn(k):
             for bank in range(ROW_TILES // 2):
@@ -399,22 +426,13 @@ def tile_snnlayer_pa_t_kernel(
                 load_x(c + 1)
                 load_mem(c + 1)
 
-        def turn_late(k):
-            if k == STEPS:
-                return
-            if k == STEPS + 1:
-                turn(STEPS)
-            turn(k)
-
-        step = ((load, 4), (quantise, 3), (threshold, 2), (reset, 2), (finish, -6), (update, -1), (decay, 0), (matmuls, 0), (offset, 1), (spike_part, 3), (turn_late, 5), (turn_back, -5), (turn_b, 4), (spread, 6))
+        step = ((load, 4), (quantise, 3), (update, -1), (decay, 0), (finish, -6), (threshold, 2), (reset, 2), (decay_rest, -2), (matmuls, 0), (offset, 0), (spike_part, 3), (turn, 5), (turn_back, -5), (turn_b, 4), (spread, 6))
         for n in range(-TURN_LEAD, UNITS + FINISH_LAG):
-            if n == -2:
-                permute_scales()
-                permute_words(0)
-                permute_words(1)
-            if n == -2 + 1:
-                permute_words(2)
-                permute_words(3)
+            for g in range(PASSES):
+                if g % 2 == 0 and n == (-2, -1)[g // 2]:
+                    permute_scales(g // 2)
+                if n == (-2, -2, -1, -1)[g]:
+                    permute_words(g)
             for stage, offset_in_units in step:
                 if live(n + offset_in_units):
                     stage(n + offset_in_units)

@@ -15,15 +15,17 @@ ACT = mybir.ActivationFunctionType
 P = 128
 SAMPLES = 4096
 NEURONS = 512
-CHUNK = 512
-ROW_TILES = CHUNK // P
-N_CHUNKS = SAMPLES // CHUNK
+ROW_TILES = (4, 4, 4, 4, 4, 4, 4, 4)
+N_CHUNKS = len(ROW_TILES)
+CHUNK = P * max(ROW_TILES)
+FIRST_TILE = [sum(ROW_TILES[:c]) for c in range(N_CHUNKS)]
+assert P * sum(ROW_TILES) == SAMPLES
 BLOCKS = NEURONS // P
 PASSES = 4
 WORDS = 256
 STEPS = 4
 UNITS = N_CHUNKS * STEPS
-assert PASSES == STEPS and BLOCKS == STEPS and ROW_TILES == STEPS
+assert PASSES == STEPS and BLOCKS == STEPS
 TURN_LEAD = STEPS + 1
 BACK_LAG = STEPS + 1
 FINISH_LAG = BACK_LAG + 1
@@ -57,11 +59,10 @@ def tile_snnlayer_pa_t_kernel(
 ):
     nc = tc.nc
 
-    x_chunks = x_t.rearrange("(c p i) k -> c p i k", p=P, i=ROW_TILES)
-    spk_chunks = spk_t.rearrange("(c p i) k -> c p i k", p=P, i=ROW_TILES)
-    mem_chunks = mem_t_in.rearrange("(c p i) n -> c p i n", p=P, i=ROW_TILES)
-    b_chunks = b_t_in.rearrange("(c p i) n -> c p i n", p=P, i=ROW_TILES)
-    out_chunks = out.rearrange("(c p i) n -> c p i n", p=P, i=ROW_TILES)
+    def rows_of(tensor, c):
+        t = ROW_TILES[c]
+        first = P * FIRST_TILE[c]
+        return tensor[first : first + P * t, :].rearrange("(p i) k -> p i k", i=t)
 
     with ExitStack() as stack:
         const = stack.enter_context(tc.tile_pool(name="const", bufs=1))
@@ -76,31 +77,42 @@ def tile_snnlayer_pa_t_kernel(
         mem_tiles = {}
         b_tiles = {}
 
-        def load_rows(c, tile, rows):
-            pieces = 1 if c == 0 else 1
-            for piece in range(pieces):
-                part = slice(piece * ROW_TILES // pieces, (piece + 1) * ROW_TILES // pieces)
-                nc.sync.dma_start(out=tile[:, part, :], in_=rows[:, part, :])
-
         def load_spk(c):
-            spk_tiles[c] = loads.tile([P, ROW_TILES, 2 * 512], BF16, tag="spk", name="spk_sb")
-            load_rows(c, spk_tiles[c], spk_chunks[c])
+            spk_tiles[c] = loads.tile([P, ROW_TILES[c], 2 * 512], BF16, tag="spk", name="spk_sb")
+            pieces = 2 if c == 0 else 1
+            for piece in range(pieces):
+                part = slice(piece * ROW_TILES[c] // pieces, (piece + 1) * ROW_TILES[c] // pieces)
+                nc.sync.dma_start(out=spk_tiles[c][:, part, :], in_=rows_of(spk_t, c)[:, part, :])
 
         def load_x(c):
-            x_tiles[c] = loads.tile([P, ROW_TILES, 2 * 512], BF16, tag="x", name="x_sb")
-            nc.sync.dma_start(out=x_tiles[c][:], in_=x_chunks[c])
+            x_tiles[c] = loads.tile([P, ROW_TILES[c], 2 * 512], BF16, tag="x", name="x_sb")
+            nc.sync.dma_start(out=x_tiles[c][:], in_=rows_of(x_t, c))
 
         def load_b(c):
-            b_tiles[c] = loads.tile([P, ROW_TILES, NEURONS], BF16, tag="b", name="b_sb")
-            nc.sync.dma_start(out=b_tiles[c][:], in_=b_chunks[c])
+            b_tiles[c] = loads.tile([P, ROW_TILES[c], NEURONS], BF16, tag="b", name="b_sb")
+            nc.sync.dma_start(out=b_tiles[c][:], in_=rows_of(b_t_in, c))
 
         def load_mem(c):
-            mem_tiles[c] = loads.tile([P, ROW_TILES, NEURONS], BF16, tag="mem", bufs=5, name="mem_sb")
-            nc.sync.dma_start(out=mem_tiles[c][:], in_=mem_chunks[c])
+            mem_tiles[c] = loads.tile([P, ROW_TILES[c], NEURONS], BF16, tag="mem", bufs=5, name="mem_sb")
+            nc.sync.dma_start(out=mem_tiles[c][:], in_=rows_of(mem_t_in, c))
 
-        vectors = [b_x2in, b_rec4in, b_out2in, tau_adp_in, tau_m_in]
-        vec_rows = const.tile([P, NEURONS], BF16)
-        nc.vector.memset(vec_rows[:], 0.0)
+        tau_m_col = const.tile([P, BLOCKS], BF16)
+        tau_adp_col = const.tile([P, BLOCKS], BF16)
+        b_x_col = const.tile([P, BLOCKS], BF16)
+        b_rec_col = const.tile([P, BLOCKS], BF16)
+        b_out_col = const.tile([P, BLOCKS], BF16)
+
+        def load_column(queue, column, vector):
+            queue.dma_start(out=column[:], in_=vector.rearrange("(m j) -> m j", j=BLOCKS))
+
+        def load_taus():
+            load_column(nc.scalar, tau_adp_col, tau_adp_in)
+            load_column(nc.scalar, tau_m_col, tau_m_in)
+
+        def load_biases():
+            load_column(nc.gpsimd, b_x_col, b_x2in)
+            load_column(nc.gpsimd, b_rec_col, b_rec4in)
+            load_column(nc.gpsimd, b_out_col, b_out2in)
 
         w_words = const.tile([P, PASSES, NEURONS], I32, align_bytes=64)
         w_planes = const.tile([P, 2, NEURONS], U8, align_bytes=64)
@@ -124,20 +136,17 @@ def tile_snnlayer_pa_t_kernel(
                     out=w_words[:, 2:4, :], in_=W_x2in_words.rearrange("g p n t -> p g (n t)").bitcast(I32)
                 )
 
-        def load_vectors():
-            for v, vector in enumerate(vectors):
-                nc.scalar.dma_start(out=vec_rows[v : v + 1, :], in_=vector.rearrange("(o n) -> o n", o=1))
-
         ident_f32 = const.tile([P, P], F32)
         make_identity(nc, ident_f32[:])
-        load_scales(0, range(4))
+        load_biases()
         load_spk(0)
-        load_vectors()
+        load_taus()
         load_b(0)
         load_x(0)
         load_words(0)
-        load_scales(1, range(4))
+        load_scales(0, range(4))
         load_words(1)
+        load_scales(1, range(4))
         load_words(2)
         load_scales(2, range(4))
         load_spk(1)
@@ -147,7 +156,6 @@ def tile_snnlayer_pa_t_kernel(
         load_x(1)
         load_mem(1)
 
-        vec_cols = const.tile([P, len(vectors), BLOCKS], F32)
         p_col = const.tile([P, BLOCKS], F32)
         a_col = const.tile([P, BLOCKS], F32)
         bias_two = const.tile([P, BLOCKS], F32)
@@ -177,26 +185,19 @@ def tile_snnlayer_pa_t_kernel(
             )
 
         def constants():
-            vec_ps = psum.tile([P, 2, P], F32, tag="turned", bufs=2, name="vec_ps")
-            vec_words = vec_rows[:].bitcast(F32)
-            for u in (0, 1):
-                nc.tensor.transpose(vec_ps[:, u, :], vec_words[:, u:WORDS:2], ident_f32[:])
-            for u in (0, 1):
-                nc.vector.tensor_copy(
-                    out=vec_cols[:, :, 2 * u : 2 * u + 2],
-                    in_=vec_ps[:, u, :].bitcast(BF16).rearrange("p (v e) -> p v e", e=2)[:, 0 : len(vectors), :],
-                )
-            nc.scalar.activation(out=p_col[:], in_=vec_cols[:, 3, :], func=ACT.Sigmoid)
-            nc.scalar.activation(out=a_col[:], in_=vec_cols[:, 4, :], func=ACT.Sigmoid)
+            nc.scalar.activation(out=p_col[:], in_=tau_adp_col[:], func=ACT.Sigmoid)
+            nc.scalar.activation(out=a_col[:], in_=tau_m_col[:], func=ACT.Sigmoid)
             nc.vector.tensor_scalar(
                 out=thre_spk[:], in0=p_col[:], scalar1=-BETA, scalar2=BETA, op0=ALU.mult, op1=ALU.add
             )
             nc.vector.tensor_scalar(out=thre_b[:], in0=p_col[:], scalar1=BETA, scalar2=None, op0=ALU.mult)
-            nc.vector.tensor_tensor(out=bias_two[:], in0=vec_cols[:, 0, :], in1=vec_cols[:, 1, :], op=ALU.add)
             nc.vector.tensor_scalar(
                 out=drive_gain[:], in0=a_col[:], scalar1=-R_M, scalar2=R_M, op0=ALU.mult, op1=ALU.add
             )
-            nc.vector.tensor_tensor(out=bias_sum[:], in0=bias_two[:], in1=vec_cols[:, 2, :], op=ALU.add)
+
+        def bias_constants():
+            nc.vector.tensor_tensor(out=bias_two[:], in0=b_x_col[:], in1=b_rec_col[:], op=ALU.add)
+            nc.vector.tensor_tensor(out=bias_sum[:], in0=bias_two[:], in1=b_out_col[:], op=ALU.add)
             nc.vector.tensor_tensor(out=drive_bias[:], in0=drive_gain[:], in1=bias_sum[:], op=ALU.mult)
 
         def decay_rows():
@@ -221,22 +222,32 @@ def tile_snnlayer_pa_t_kernel(
         decay_tiles = {}
         back_tiles = {}
 
+        def row_tile(k):
+            c, q = divmod(k, STEPS)
+            i, rest = divmod(q * ROW_TILES[c], STEPS)
+            return (c, i) if rest == 0 else None
+
         def turn_half(k, bank):
             c, g = divmod(k, PASSES)
             source = (spk_tiles[c] if g < 2 else x_tiles[c])[:].bitcast(F32)
             first_word = (WORDS, 0, 0, WORDS)[g]
-            if k < PASSES and bank == 1:
+            if k < PASSES and (bank == 1 or k % 2 == 1):
                 turned = psum.tile([P, 2, 2 * P], F32, tag="sums", name="turned_first")
             else:
                 turned = psum.tile([P, 2, 2 * P], F32, tag="turned", bufs=2, name="turned")
             for i in (0, 1):
                 for u in (0, 1):
-                    if bank == 1 and k in spread_tiles:
-                        words = spread_tiles[k][:, i, u, :]
+                    row = 2 * bank + i
+                    apart = row - spread_first(k)
+                    if apart >= 0 and k in spread_tiles:
+                        words = spread_tiles[k][:, apart, u, :]
                     else:
-                        words = source[:, 2 * bank + i, first_word + u : first_word + WORDS : 2]
+                        words = source[:, row, first_word + u : first_word + WORDS : 2]
                     nc.tensor.transpose(turned[:, u, P * i : P * (i + 1)], words, ident_f32[:])
             turned_tiles[k] = turned
+
+        def spread_first(k):
+            return 2
 
         def spread(k):
             if k < SPREAD_FROM:
@@ -244,17 +255,18 @@ def tile_snnlayer_pa_t_kernel(
             c, g = divmod(k, PASSES)
             source = (spk_tiles[c] if g < 2 else x_tiles[c])[:].bitcast(F32)
             first_word = (WORDS, 0, 0, WORDS)[g]
-            spread_tiles[k] = quant.tile([P, 2, 2, P], F32, tag="spread", bufs=3, name="spread_words")
+            half = spread_first(k)
+            spread_tiles[k] = quant.tile([P, ROW_TILES[c] - half, 2, P], F32, tag="spread", bufs=3, name="spread_words")
             nc.scalar.copy(
                 out=spread_tiles[k][:],
-                in_=source[:, 2:4, first_word : first_word + WORDS].rearrange("p i (w u) -> p i u w", u=2),
+                in_=source[:, half:, first_word : first_word + WORDS].rearrange("p i (w u) -> p i u w", u=2),
             )
 
         def group_half(k, bank):
             if bank == 0:
                 spike = k % PASSES == 0
                 grouped_tiles[k] = quant.tile(
-                    [P, 4 * CHUNK],
+                    [P, 4 * P * ROW_TILES[k // PASSES]],
                     BF16,
                     tag="grouped_in" if spike else "grouped",
                     bufs=3,
@@ -262,7 +274,7 @@ def tile_snnlayer_pa_t_kernel(
                     align_bytes=64,
                 )
             words = grouped_tiles[k][:].bitcast(F32).rearrange("p (s u) -> p s u", u=2)
-            copy = nc.vector.tensor_copy if k < 2 and bank == 1 else nc.scalar.copy
+            copy = nc.vector.tensor_copy if k in (0, 1) and bank == ROW_TILES[0] // 2 - 1 else nc.scalar.copy
             copy(
                 out=words[:, 2 * P * bank : 2 * P * (bank + 1), :], in_=turned_tiles[k][:].rearrange("p u s -> p s u")
             )
@@ -270,8 +282,9 @@ def tile_snnlayer_pa_t_kernel(
         def quantise(k):
             c, g = divmod(k, PASSES)
             if g == 0:
-                codes_tiles[c] = quant.tile([P, PASSES, CHUNK], U32, tag="codes", name="codes", align_bytes=64)
-                planes_tiles[c] = quant.tile([P, PASSES, CHUNK], U8, tag="planes", name="planes", align_bytes=64)
+                samples = P * ROW_TILES[c]
+                codes_tiles[c] = quant.tile([P, PASSES, samples], U32, tag="codes", name="codes", align_bytes=64)
+                planes_tiles[c] = quant.tile([P, PASSES, samples], U8, tag="planes", name="planes", align_bytes=64)
             nc.vector.quantize_mx(
                 out=codes_tiles[c][:, g, :].bitcast(FP8X4), scales=planes_tiles[c][:, g, :], in_=grouped_tiles[k][:]
             )
@@ -284,16 +297,16 @@ def tile_snnlayer_pa_t_kernel(
             c, q = divmod(k, STEPS)
             u, half = divmod(q, 2)
             if half == 0:
-                b_turned_tiles[(c, u)] = psum.tile([P, CHUNK], F32, tag="b_turned", name="b_turned")
+                b_turned_tiles[(c, u)] = psum.tile([P, P * ROW_TILES[c]], F32, tag="b_turned", name="b_turned")
             source = b_tiles[c][:].bitcast(F32)
-            for i in (2 * half, 2 * half + 1):
+            for i in range(half * ROW_TILES[c] // 2, (half + 1) * ROW_TILES[c] // 2):
                 nc.tensor.transpose(
                     b_turned_tiles[(c, u)][:, P * i : P * (i + 1)], source[:, i, u:WORDS:2], ident_f32[:]
                 )
 
         def spike_part(k):
             j = k % BLOCKS
-            part = work.tile([P, CHUNK], F32, tag="spk_part", name="spk_part")
+            part = work.tile([P, P * ROW_TILES[k // STEPS]], F32, tag="spk_part", name="spk_part")
             nc.scalar.activation(
                 out=part[:], in_=spikes(k), func=ACT.Identity, scale=thre_spk[:, j : j + 1], bias=baseline[:]
             )
@@ -302,7 +315,7 @@ def tile_snnlayer_pa_t_kernel(
         def threshold(k):
             c, j = divmod(k, BLOCKS)
             turned = b_turned_tiles[(c, j // 2)][:].bitcast(BF16).rearrange("p (s e) -> p e s", e=2)
-            thre = work.tile([P, CHUNK], F32, tag="thre", name="thre")
+            thre = work.tile([P, P * ROW_TILES[k // STEPS]], F32, tag="thre", name="thre")
             nc.vector.scalar_tensor_tensor(
                 out=thre[:],
                 in0=turned[:, j % 2, :],
@@ -314,13 +327,13 @@ def tile_snnlayer_pa_t_kernel(
             thre_tiles[k] = thre
 
         def reset(k):
-            product = work.tile([P, CHUNK], F32, tag="reset", name="reset")
+            product = work.tile([P, P * ROW_TILES[k // STEPS]], F32, tag="reset", name="reset")
             nc.gpsimd.tensor_tensor(out=product[:], in0=thre_tiles[k][:], in1=spikes(k), op=ALU.mult)
             reset_tiles[k] = product
 
         def offset(k):
             j = k % BLOCKS
-            part = work.tile([P, CHUNK], F32, tag="offset", name="offset")
+            part = work.tile([P, P * ROW_TILES[k // STEPS]], F32, tag="offset", name="offset")
             nc.scalar.activation(
                 out=part[:], in_=reset_tiles[k][:], func=ACT.Identity, scale=-1.0, bias=drive_bias[:, j : j + 1]
             )
@@ -329,7 +342,7 @@ def tile_snnlayer_pa_t_kernel(
         def matmuls(k):
             c, j = divmod(k, BLOCKS)
             neurons = slice(P * j, P * (j + 1))
-            sums_tiles[k] = psum.tile([P, CHUNK], F32, tag="sums", name="sums")
+            sums_tiles[k] = psum.tile([P, P * ROW_TILES[c]], F32, tag="sums", name="sums")
             for g in range(PASSES):
                 nc.tensor.matmul_mx(
                     out=sums_tiles[k][:],
@@ -343,7 +356,7 @@ def tile_snnlayer_pa_t_kernel(
 
         def update(k):
             j = k % BLOCKS
-            part = work.tile([P, CHUNK], F32, tag="update", bufs=10, name="update")
+            part = work.tile([P, P * ROW_TILES[k // STEPS]], F32, tag="update", bufs=10, name="update")
             nc.vector.scalar_tensor_tensor(
                 out=part[:],
                 in0=sums_tiles[k][:],
@@ -355,9 +368,11 @@ def tile_snnlayer_pa_t_kernel(
             update_tiles[k] = part
 
         def decay(k):
-            c, i = divmod(k, ROW_TILES)
+            if not row_tile(k):
+                return
+            c, i = row_tile(k)
             decay_tiles[k] = work.tile([P, NEURONS], F32, tag="decayed", bufs=8, name="decayed")
-            cols = 0 if k >= UNITS - ROW_TILES else NEURONS
+            cols = 0 if k >= UNITS - 4 else NEURONS - 128
             if cols == 0:
                 return
             nc.vector.tensor_tensor(
@@ -368,8 +383,10 @@ def tile_snnlayer_pa_t_kernel(
             )
 
         def decay_rest(k):
-            c, i = divmod(k, ROW_TILES)
-            cols = 0 if k >= UNITS - ROW_TILES else NEURONS
+            if not row_tile(k):
+                return
+            c, i = row_tile(k)
+            cols = 0 if k >= UNITS - 4 else NEURONS - 128
             if cols == NEURONS:
                 return
             nc.gpsimd.tensor_tensor(
@@ -380,10 +397,12 @@ def tile_snnlayer_pa_t_kernel(
             )
 
         def turn_back(k):
-            c, i = divmod(k, ROW_TILES)
-            if k < UNITS - 2 * ROW_TILES or (k < UNITS - ROW_TILES and k % 2 == 1):
+            if not row_tile(k):
+                return
+            c, i = row_tile(k)
+            if k < UNITS - 2 * STEPS or (k < UNITS - STEPS and k % 2 == 1):
                 back = psum.tile([P, NEURONS], F32, tag="back", bufs=1, name="back")
-            elif k % 2 == 0:
+            elif i % 2 == 0:
                 back = psum.tile([P, NEURONS], F32, tag="turned", bufs=2, name="back_last")
             else:
                 back = psum.tile([P, NEURONS], F32, tag="b_turned", name="back_last")
@@ -396,9 +415,11 @@ def tile_snnlayer_pa_t_kernel(
             back_tiles[k] = back
 
         def finish(k):
-            c, i = divmod(k, ROW_TILES)
+            if not row_tile(k):
+                return
+            c, i = row_tile(k)
             result = work.tile([P, NEURONS], F32, tag="result", bufs=8, name="result")
-            pieces = 2 if k == UNITS - 1 else 1
+            pieces = 2 if (c, i) == (N_CHUNKS - 1, ROW_TILES[-1] - 1) else 1
             for piece in range(pieces):
                 cols = slice(piece * P // pieces, (piece + 1) * P // pieces)
                 ncols = slice(piece * NEURONS // pieces, (piece + 1) * NEURONS // pieces)
@@ -408,10 +429,10 @@ def tile_snnlayer_pa_t_kernel(
                     in1=decay_tiles[k][:].rearrange("p (m j) -> p m j", j=BLOCKS)[:, cols, :],
                     op=ALU.add,
                 )
-                nc.sync.dma_start(out=out_chunks[c][:, i, ncols], in_=result[:, ncols])
+                nc.sync.dma_start(out=rows_of(out, c)[:, i, ncols], in_=result[:, ncols])
 
         def turn(k):
-            for bank in range(ROW_TILES // 2):
+            for bank in range(ROW_TILES[k // STEPS] // 2):
                 turn_half(k, bank)
                 group_half(k, bank)
 
@@ -426,7 +447,8 @@ def tile_snnlayer_pa_t_kernel(
                 load_x(c + 1)
                 load_mem(c + 1)
 
-        step = ((load, 4), (quantise, 3), (update, -1), (decay, 0), (finish, -6), (threshold, 2), (reset, 2), (decay_rest, -2), (matmuls, 0), (offset, 0), (spike_part, 3), (turn, 5), (turn_back, -5), (turn_b, 4), (spread, 6))
+        step = ((load, 4), (quantise, 3), (update, -1), (decay, 0), (finish, -6), (threshold, 2), (reset, 2), (decay_rest, -1), (matmuls, 0), (offset, 0), (spike_part, 3), (turn, 5), (turn_back, -5), (turn_b, 4), (spread, 6))
+        constants()
         for n in range(-TURN_LEAD, UNITS + FINISH_LAG):
             for g in range(PASSES):
                 if g % 2 == 0 and n == (-2, -1)[g // 2]:
@@ -436,7 +458,6 @@ def tile_snnlayer_pa_t_kernel(
             for stage, offset_in_units in step:
                 if live(n + offset_in_units):
                     stage(n + offset_in_units)
-            if n == -TURN_LEAD:
-                constants()
             if n == -TURN_LEAD + 2:
                 decay_rows()
+                bias_constants()

@@ -164,8 +164,6 @@ def tile_snnlayer_pa_t_kernel(
         drive_bias = const.tile([P, BLOCKS], F32)
         thre_b = const.tile([P, BLOCKS], F32)
         thre_spk = const.tile([P, BLOCKS], F32)
-        baseline = const.tile([P, 1], F32)
-        nc.vector.memset(baseline[:], BASELINE_THRE)
         a_rows = psum.tile([P, NEURONS], F32, tag="a_rows", bufs=1)
         a_rows_sb = const.tile([P, NEURONS], F32)
 
@@ -247,7 +245,7 @@ def tile_snnlayer_pa_t_kernel(
             turned_tiles[k] = turned
 
         def spread_first(k):
-            return 2
+            return 2 + k % 2
 
         def spread(k):
             if k < SPREAD_FROM:
@@ -308,7 +306,7 @@ def tile_snnlayer_pa_t_kernel(
             j = k % BLOCKS
             part = work.tile([P, P * ROW_TILES[k // STEPS]], F32, tag="spk_part", name="spk_part")
             nc.scalar.activation(
-                out=part[:], in_=spikes(k), func=ACT.Identity, scale=thre_spk[:, j : j + 1], bias=baseline[:]
+                out=part[:], in_=spikes(k), func=ACT.Identity, scale=thre_spk[:, j : j + 1], bias=BASELINE_THRE
             )
             spk_part_tiles[k] = part
 

@@ -27,9 +27,9 @@ STEPS = 4
 UNITS = N_CHUNKS * STEPS
 assert PASSES == STEPS and BLOCKS == STEPS
 TURN_LEAD = STEPS + 1
-BACK_LAG = STEPS + 1
-FINISH_LAG = BACK_LAG + 1
-SPREAD_FROM = 8
+BACK_LAG = 5
+FINISH_LAG = 6
+SPREAD_FROM = 12
 
 BASELINE_THRE = 0.1
 BETA = 1.8
@@ -272,7 +272,7 @@ def tile_snnlayer_pa_t_kernel(
                     align_bytes=64,
                 )
             words = grouped_tiles[k][:].bitcast(F32).rearrange("p (s u) -> p s u", u=2)
-            copy = nc.vector.tensor_copy if k in (0, 1) and bank == ROW_TILES[0] // 2 - 1 else nc.scalar.copy
+            copy = nc.vector.tensor_copy if k in () and bank == ROW_TILES[0] // 2 - 1 else nc.scalar.copy
             copy(
                 out=words[:, 2 * P * bank : 2 * P * (bank + 1), :], in_=turned_tiles[k][:].rearrange("p u s -> p s u")
             )
@@ -445,7 +445,7 @@ def tile_snnlayer_pa_t_kernel(
                 load_x(c + 1)
                 load_mem(c + 1)
 
-        step = ((load, 4), (quantise, 3), (update, -1), (decay, 0), (finish, -6), (threshold, 2), (reset, 2), (decay_rest, -1), (matmuls, 0), (offset, 0), (spike_part, 3), (turn, 5), (turn_back, -5), (turn_b, 4), (spread, 6))
+        step = ((load, 4), (quantise, 3), (update, -1), (decay, 0), (finish, -6), (threshold, 2), (reset, 2), (decay_rest, -1), (matmuls, 0), (offset, 0), (spike_part, 3), (turn, 5), (turn_back, -5), (turn_b, 4), (spread, 7))
         constants()
         for n in range(-TURN_LEAD, UNITS + FINISH_LAG):
             for g in range(PASSES):

@@ -30,6 +30,7 @@ TURN_LEAD = STEPS + 1
 BACK_LAG = 5
 FINISH_LAG = 6
 SPREAD_FROM = 12
+EARLY_UNITS = 2
 
 BASELINE_THRE = 0.1
 BETA = 1.8
@@ -338,10 +339,22 @@ def tile_snnlayer_pa_t_kernel(
             offset_tiles[k] = part
 
         def matmuls(k):
+            if k >= EARLY_UNITS:
+                matmul_passes(k, range(PASSES))
+            else:
+                matmul_passes(k, range(2, PASSES))
+
+        def early_matmuls(k):
+            if k == 0:
+                for unit in range(EARLY_UNITS):
+                    matmul_passes(unit, range(2))
+
+        def matmul_passes(k, passes):
             c, j = divmod(k, BLOCKS)
             neurons = slice(P * j, P * (j + 1))
-            sums_tiles[k] = psum.tile([P, P * ROW_TILES[c]], F32, tag="sums", name="sums")
-            for g in range(PASSES):
+            if 0 in passes:
+                sums_tiles[k] = psum.tile([P, P * ROW_TILES[c]], F32, tag="sums", name="sums")
+            for g in passes:
                 nc.tensor.matmul_mx(
                     out=sums_tiles[k][:],
                     lhsT=w_codes[:, g, neurons].bitcast(FP8X4),
@@ -437,6 +450,12 @@ def tile_snnlayer_pa_t_kernel(
         def live(k):
             return 0 <= k < UNITS
 
+        def permute(k):
+            if k < 2:
+                permute_scales(k)
+                permute_words(2 * k)
+                permute_words(2 * k + 1)
+
         def load(k):
             c, q = divmod(k, STEPS)
             if q == 0 and 0 < c < N_CHUNKS - 1:
@@ -445,14 +464,9 @@ def tile_snnlayer_pa_t_kernel(
                 load_x(c + 1)
                 load_mem(c + 1)
 
-        step = ((load, 4), (quantise, 3), (update, -1), (decay, 0), (finish, -6), (threshold, 2), (reset, 2), (decay_rest, -1), (matmuls, 0), (offset, 0), (spike_part, 3), (turn, 5), (turn_back, -5), (turn_b, 4), (spread, 7))
+        step = ((load, 4), (quantise, 3), (permute, 2), (update, -1), (decay, 0), (finish, -6), (threshold, 2), (reset, 2), (decay_rest, -1), (matmuls, 0), (offset, 0), (spike_part, 3), (early_matmuls, 1), (turn, 5), (turn_back, -5), (turn_b, 4), (spread, 7))
         constants()
         for n in range(-TURN_LEAD, UNITS + FINISH_LAG):
-            for g in range(PASSES):
-                if g % 2 == 0 and n == (-2, -1)[g // 2]:
-                    permute_scales(g // 2)
-                if n == (-2, -2, -1, -1)[g]:
-                    permute_words(g)
             for stage, offset_in_units in step:
                 if live(n + offset_in_units):
                     stage(n + offset_in_units)

from contextlib import ExitStack

import concourse.mybir as mybir
from concourse.masks import make_identity

F32 = mybir.dt.float32
BF16 = mybir.dt.bfloat16
I32 = mybir.dt.int32
U32 = mybir.dt.uint32
U8 = mybir.dt.uint8
FP8X4 = mybir.dt.float8_e4m3fn_x4
ALU = mybir.AluOpType
ACT = mybir.ActivationFunctionType

P = 128
SAMPLES = 4096
NEURONS = 512
ROW_TILES = (4, 4, 4, 4, 4, 4, 4, 4)
N_CHUNKS = len(ROW_TILES)
CHUNK = P * max(ROW_TILES)
FIRST_TILE = [sum(ROW_TILES[:c]) for c in range(N_CHUNKS)]
assert P * sum(ROW_TILES) == SAMPLES
BLOCKS = NEURONS // P
PASSES = 4
WORDS = 256
STEPS = 4
UNITS = N_CHUNKS * STEPS
assert PASSES == STEPS and BLOCKS == STEPS
TURN_LEAD = STEPS + 1
BACK_LAG = 5
FINISH_LAG = 6
SPREAD_FROM = 12
EARLY_UNITS = 2

BASELINE_THRE = 0.1
BETA = 1.8
R_M = 3.0

FLOPS = 2 * SAMPLES * (PASSES * 512) * NEURONS


def tile_snnlayer_pa_t_kernel(
    tc,
    x_t,
    spk_t,
    mem_t_in,
    b_t_in,
    W_x2in_words,
    W_x2in_scales,
    b_x2in,
    W_rec4in_words,
    W_rec4in_scales,
    b_rec4in,
    W_out2in_words,
    W_out2in_scales,
    b_out2in,
    tau_adp_in,
    tau_m_in,
    out,
):
    nc = tc.nc

    def rows_of(tensor, c):
        t = ROW_TILES[c]
        first = P * FIRST_TILE[c]
        return tensor[first : first + P * t, :].rearrange("(p i) k -> p i k", i=t)

    with ExitStack() as stack:
        const = stack.enter_context(tc.tile_pool(name="const", bufs=1))
        loads = stack.enter_context(tc.tile_pool(name="loads", bufs=3))
        quant = stack.enter_context(tc.tile_pool(name="quant", bufs=2))
        work = stack.enter_context(tc.tile_pool(name="work", bufs=4))
        psum = stack.enter_context(tc.psum_pool(name="psum", bufs=2))
        stack.enter_context(tc.manual_schedule())

        x_tiles = {}
        spk_tiles = {}
        mem_tiles = {}
        b_tiles = {}

        def load_spk(c):
            spk_tiles[c] = loads.tile([P, ROW_TILES[c], 2 * 512], BF16, tag="spk", name="spk_sb")
            pieces = 2 if c == 0 else 1
            for piece in range(pieces):
                part = slice(piece * ROW_TILES[c] // pieces, (piece + 1) * ROW_TILES[c] // pieces)
                nc.sync.dma_start(out=spk_tiles[c][:, part, :], in_=rows_of(spk_t, c)[:, part, :])

        def load_x(c):
            x_tiles[c] = loads.tile([P, ROW_TILES[c], 2 * 512], BF16, tag="x", name="x_sb")
            nc.sync.dma_start(out=x_tiles[c][:], in_=rows_of(x_t, c))

        def load_b(c):
            b_tiles[c] = loads.tile([P, ROW_TILES[c], NEURONS], BF16, tag="b", name="b_sb")
            nc.sync.dma_start(out=b_tiles[c][:], in_=rows_of(b_t_in, c))

        def load_mem(c):
            mem_tiles[c] = loads.tile([P, ROW_TILES[c], NEURONS], BF16, tag="mem", bufs=5, name="mem_sb")
            nc.sync.dma_start(out=mem_tiles[c][:], in_=rows_of(mem_t_in, c))

        tau_m_col = const.tile([P, BLOCKS], BF16)
        tau_adp_col = const.tile([P, BLOCKS], BF16)
        b_x_col = const.tile([P, BLOCKS], BF16)
        b_rec_col = const.tile([P, BLOCKS], BF16)
        b_out_col = const.tile([P, BLOCKS], BF16)

        def load_column(queue, column, vector):
            queue.dma_start(out=column[:], in_=vector.rearrange("(m j) -> m j", j=BLOCKS))

        def load_taus():
            load_column(nc.scalar, tau_adp_col, tau_adp_in)
            load_column(nc.scalar, tau_m_col, tau_m_in)

        def load_biases():
            load_column(nc.gpsimd, b_x_col, b_x2in)
            load_column(nc.gpsimd, b_rec_col, b_rec4in)
            load_column(nc.gpsimd, b_out_col, b_out2in)

        w_words = const.tile([P, PASSES, NEURONS], I32, align_bytes=64)
        w_planes = const.tile([P, 2, NEURONS], U8, align_bytes=64)
        nc.vector.memset(w_planes[:].rearrange("p h n -> p (h n)").bitcast(I32), 0)

        def load_scales(g, quadrants):
            source = (W_rec4in_scales[0], W_out2in_scales[0], W_x2in_scales[0], W_x2in_scales[1])[g]
            for quadrant in quadrants:
                first = 32 * quadrant + 4 * (g % 2)
                nc.sync.dma_start(
                    out=w_planes[first : first + 4, g // 2, :].bitcast(I32),
                    in_=source[4 * quadrant : 4 * quadrant + 4, :].bitcast(I32),
                )

        def load_words(g):
            if g < 2:
                source = (W_rec4in_words, W_out2in_words)[g]
                nc.sync.dma_start(out=w_words[:, g, :], in_=source[0].rearrange("p n t -> p (n t)").bitcast(I32))
            else:
                nc.sync.dma_start(
                    out=w_words[:, 2:4, :], in_=W_x2in_words.rearrange("g p n t -> p g (n t)").bitcast(I32)
                )

        ident_f32 = const.tile([P, P], F32)
        make_identity(nc, ident_f32[:])
        load_biases()
        load_spk(0)
        load_taus()
        load_b(0)
        load_x(0)
        load_words(0)
        load_scales(0, range(4))
        load_words(1)
        load_scales(1, range(4))
        load_words(2)
        load_scales(2, range(4))
        load_spk(1)
        load_scales(3, range(4))
        load_b(1)
        load_mem(0)
        load_x(1)
        load_mem(1)

        p_col = const.tile([P, BLOCKS], F32)
        a_col = const.tile([P, BLOCKS], F32)
        bias_two = const.tile([P, BLOCKS], F32)
        bias_sum = const.tile([P, BLOCKS], F32)
        drive_gain = const.tile([P, BLOCKS], F32)
        drive_bias = const.tile([P, BLOCKS], F32)
        thre_b = const.tile([P, BLOCKS], F32)
        thre_spk = const.tile([P, BLOCKS], F32)
        a_rows = psum.tile([P, NEURONS], F32, tag="a_rows", bufs=1)
        a_rows_sb = const.tile([P, NEURONS], F32)

        w_codes = const.tile([P, PASSES, NEURONS], I32, align_bytes=64)
        w_scales = const.tile([P, 2, NEURONS], U8, align_bytes=64)

        def permute_scales(half):
            nc.vector.tensor_copy(
                out=w_scales[:, half, :].rearrange("p (j m) -> p m j", j=BLOCKS),
                in_=w_planes[:, half, :].rearrange("p (m j) -> p m j", j=BLOCKS),
            )

        def permute_words(g):
            nc.vector.tensor_copy(
                out=w_codes[:, g, :].rearrange("p (j m) -> p j m", j=BLOCKS),
                in_=w_words[:, g, :].rearrange("p (m j) -> p j m", j=BLOCKS),
            )

        def constants():
            nc.scalar.activation(out=p_col[:], in_=tau_adp_col[:], func=ACT.Sigmoid)
            nc.scalar.activation(out=a_col[:], in_=tau_m_col[:], func=ACT.Sigmoid)
            nc.vector.tensor_scalar(
                out=thre_spk[:], in0=p_col[:], scalar1=-BETA, scalar2=BETA, op0=ALU.mult, op1=ALU.add
            )
            nc.vector.tensor_scalar(out=thre_b[:], in0=p_col[:], scalar1=BETA, scalar2=None, op0=ALU.mult)
            nc.vector.tensor_scalar(
                out=drive_gain[:], in0=a_col[:], scalar1=-R_M, scalar2=R_M, op0=ALU.mult, op1=ALU.add
            )

        def bias_constants():
            nc.vector.tensor_tensor(out=bias_two[:], in0=b_x_col[:], in1=b_rec_col[:], op=ALU.add)
            nc.vector.tensor_tensor(out=bias_sum[:], in0=bias_two[:], in1=b_out_col[:], op=ALU.add)
            nc.vector.tensor_tensor(out=drive_bias[:], in0=drive_gain[:], in1=bias_sum[:], op=ALU.mult)

        def decay_rows():
            for j in range(BLOCKS):
                nc.tensor.transpose(
                    a_rows[:, P * j : P * (j + 1)], a_col[:, j : j + 1].to_broadcast([P, P]), ident_f32[:]
                )
            nc.scalar.copy(out=a_rows_sb[:], in_=a_rows[:])

        turned_tiles = {}
        spread_tiles = {}
        grouped_tiles = {}
        codes_tiles = {}
        planes_tiles = {}
        b_turned_tiles = {}
        sums_tiles = {}
        spk_part_tiles = {}
        thre_tiles = {}
        reset_tiles = {}
        offset_tiles = {}
        update_tiles = {}
        decay_tiles = {}
        back_tiles = {}

        def row_tile(k):
            c, q = divmod(k, STEPS)
            i, rest = divmod(q * ROW_TILES[c], STEPS)
            return (c, i) if rest == 0 else None

        def turn_half(k, bank):
            c, g = divmod(k, PASSES)
            source = (spk_tiles[c] if g < 2 else x_tiles[c])[:].bitcast(F32)
            first_word = (WORDS, 0, 0, WORDS)[g]
            if k < PASSES and (bank == 1 or k % 2 == 1):
                turned = psum.tile([P, 2, 2 * P], F32, tag="sums", name="turned_first")
            else:
                turned = psum.tile([P, 2, 2 * P], F32, tag="turned", bufs=2, name="turned")
            for i in (0, 1):
                for u in (0, 1):
                    row = 2 * bank + i
                    apart = row - spread_first(k)
                    if apart >= 0 and k in spread_tiles:
                        words = spread_tiles[k][:, apart, u, :]
                    else:
                        words = source[:, row, first_word + u : first_word + WORDS : 2]
                    nc.tensor.transpose(turned[:, u, P * i : P * (i + 1)], words, ident_f32[:])
            turned_tiles[k] = turned

        def spread_first(k):
            return 2 + k % 2

        def spread(k):
            if k < SPREAD_FROM:
                return
            c, g = divmod(k, PASSES)
            source = (spk_tiles[c] if g < 2 else x_tiles[c])[:].bitcast(F32)
            first_word = (WORDS, 0, 0, WORDS)[g]
            half = spread_first(k)
            spread_tiles[k] = quant.tile([P, ROW_TILES[c] - half, 2, P], F32, tag="spread", bufs=3, name="spread_words")
            nc.scalar.copy(
                out=spread_tiles[k][:],
                in_=source[:, half:, first_word : first_word + WORDS].rearrange("p i (w u) -> p i u w", u=2),
            )

        def group_half(k, bank):
            if bank == 0:
                spike = k % PASSES == 0
                grouped_tiles[k] = quant.tile(
                    [P, 4 * P * ROW_TILES[k // PASSES]],
                    BF16,
                    tag="grouped_in" if spike else "grouped",
                    bufs=3,
                    name="grouped",
                    align_bytes=64,
                )
            words = grouped_tiles[k][:].bitcast(F32).rearrange("p (s u) -> p s u", u=2)
            copy = nc.vector.tensor_copy if k in () and bank == ROW_TILES[0] // 2 - 1 else nc.scalar.copy
            copy(
                out=words[:, 2 * P * bank : 2 * P * (bank + 1), :], in_=turned_tiles[k][:].rearrange("p u s -> p s u")
            )

        def quantise(k):
            c, g = divmod(k, PASSES)
            if g == 0:
                samples = P * ROW_TILES[c]
                codes_tiles[c] = quant.tile([P, PASSES, samples], U32, tag="codes", name="codes", align_bytes=64)
                planes_tiles[c] = quant.tile([P, PASSES, samples], U8, tag="planes", name="planes", align_bytes=64)
            nc.vector.quantize_mx(
                out=codes_tiles[c][:, g, :].bitcast(FP8X4), scales=planes_tiles[c][:, g, :], in_=grouped_tiles[k][:]
            )

        def spikes(k):
            c, j = divmod(k, BLOCKS)
            return grouped_tiles[PASSES * c][:].rearrange("p (s t) -> p t s", t=4)[:, j, :]

        def turn_b(k):
            c, q = divmod(k, STEPS)
            u, half = divmod(q, 2)
            if half == 0:
                b_turned_tiles[(c, u)] = psum.tile([P, P * ROW_TILES[c]], F32, tag="b_turned", name="b_turned")
            source = b_tiles[c][:].bitcast(F32)
            for i in range(half * ROW_TILES[c] // 2, (half + 1) * ROW_TILES[c] // 2):
                nc.tensor.transpose(
                    b_turned_tiles[(c, u)][:, P * i : P * (i + 1)], source[:, i, u:WORDS:2], ident_f32[:]
                )

        def spike_part(k):
            j = k % BLOCKS
            part = work.tile([P, P * ROW_TILES[k // STEPS]], F32, tag="spk_part", name="spk_part")
            nc.scalar.activation(
                out=part[:], in_=spikes(k), func=ACT.Identity, scale=thre_spk[:, j : j + 1], bias=BASELINE_THRE
            )
            spk_part_tiles[k] = part

        def threshold(k):
            c, j = divmod(k, BLOCKS)
            turned = b_turned_tiles[(c, j // 2)][:].bitcast(BF16).rearrange("p (s e) -> p e s", e=2)
            thre = work.tile([P, P * ROW_TILES[k // STEPS]], F32, tag="thre", name="thre")
            nc.vector.scalar_tensor_tensor(
                out=thre[:],
                in0=turned[:, j % 2, :],
                scalar=thre_b[:, j : j + 1],
                in1=spk_part_tiles[k][:],
                op0=ALU.mult,
                op1=ALU.add,
            )
            thre_tiles[k] = thre

        def reset(k):
            product = work.tile([P, P * ROW_TILES[k // STEPS]], F32, tag="reset", name="reset")
            nc.gpsimd.tensor_tensor(out=product[:], in0=thre_tiles[k][:], in1=spikes(k), op=ALU.mult)
            reset_tiles[k] = product

        def offset(k):
            j = k % BLOCKS
            part = work.tile([P, P * ROW_TILES[k // STEPS]], F32, tag="offset", name="offset")
            nc.scalar.activation(
                out=part[:], in_=reset_tiles[k][:], func=ACT.Identity, scale=-1.0, bias=drive_bias[:, j : j + 1]
            )
            offset_tiles[k] = part

        def matmuls(k):
            if k >= EARLY_UNITS:
                matmul_passes(k, range(PASSES))
            else:
                matmul_passes(k, range(2, PASSES))

        def early_matmuls(k):
            if k == 0:
                for unit in range(EARLY_UNITS):
                    matmul_passes(unit, range(2))

        def matmul_passes(k, passes):
            c, j = divmod(k, BLOCKS)
            neurons = slice(P * j, P * (j + 1))
            if 0 in passes:
                sums_tiles[k] = psum.tile([P, P * ROW_TILES[c]], F32, tag="sums", name="sums")
            for g in passes:
                nc.tensor.matmul_mx(
                    out=sums_tiles[k][:],
                    lhsT=w_codes[:, g, neurons].bitcast(FP8X4),
                    lhsT_scale=w_scales[4 * (g % 2) : P, g // 2, neurons],
                    rhs=codes_tiles[c][:, g, :].bitcast(FP8X4),
                    rhs_scale=planes_tiles[c][:, g, :],
                    start=(g == 0),
                    stop=(g == PASSES - 1),
                )

        def update(k):
            j = k % BLOCKS
            part = work.tile([P, P * ROW_TILES[k // STEPS]], F32, tag="update", bufs=10, name="update")
            nc.vector.scalar_tensor_tensor(
                out=part[:],
                in0=sums_tiles[k][:],
                scalar=drive_gain[:, j : j + 1],
                in1=offset_tiles[k][:],
                op0=ALU.mult,
                op1=ALU.add,
            )
            update_tiles[k] = part

        def decay(k):
            if not row_tile(k):
                return
            c, i = row_tile(k)
            decay_tiles[k] = work.tile([P, NEURONS], F32, tag="decayed", bufs=8, name="decayed")
            cols = 0 if k >= UNITS - 4 else NEURONS - 128
            if cols == 0:
                return
            nc.vector.tensor_tensor(
                out=decay_tiles[k][:, 0:cols].rearrange("p (m j) -> p m j", j=BLOCKS),
                in0=mem_tiles[c][:, i, 0:cols].rearrange("p (m j) -> p m j", j=BLOCKS),
                in1=a_rows[:].rearrange("p (j m) -> p m j", j=BLOCKS)[:, 0 : cols // BLOCKS, :],
                op=ALU.mult,
            )

        def decay_rest(k):
            if not row_tile(k):
                return
            c, i = row_tile(k)
            cols = 0 if k >= UNITS - 4 else NEURONS - 128
            if cols == NEURONS:
                return
            nc.gpsimd.tensor_tensor(
                out=decay_tiles[k][:, cols:].rearrange("p (m j) -> p m j", j=BLOCKS),
                in0=mem_tiles[c][:, i, cols:].rearrange("p (m j) -> p m j", j=BLOCKS),
                in1=a_rows_sb[:].rearrange("p (j m) -> p m j", j=BLOCKS)[:, cols // BLOCKS :, :],
                op=ALU.mult,
            )

        def turn_back(k):
            if not row_tile(k):
                return
            c, i = row_tile(k)
            if k < UNITS - 2 * STEPS or (k < UNITS - STEPS and k % 2 == 1):
                back = psum.tile([P, NEURONS], F32, tag="back", bufs=1, name="back")
            elif i % 2 == 0:
                back = psum.tile([P, NEURONS], F32, tag="turned", bufs=2, name="back_last")
            else:
                back = psum.tile([P, NEURONS], F32, tag="b_turned", name="back_last")
            for j in range(BLOCKS):
                nc.tensor.transpose(
                    back[:, P * j : P * (j + 1)],
                    update_tiles[BLOCKS * c + j][:, P * i : P * (i + 1)],
                    ident_f32[:],
                )
            back_tiles[k] = back

        def finish(k):
            if not row_tile(k):
                return
            c, i = row_tile(k)
            result = work.tile([P, NEURONS], F32, tag="result", bufs=8, name="result")
            pieces = 2 if (c, i) == (N_CHUNKS - 1, ROW_TILES[-1] - 1) else 1
            for piece in range(pieces):
                cols = slice(piece * P // pieces, (piece + 1) * P // pieces)
                ncols = slice(piece * NEURONS // pieces, (piece + 1) * NEURONS // pieces)
                nc.vector.tensor_tensor(
                    out=result[:].rearrange("p (m j) -> p m j", j=BLOCKS)[:, cols, :],
                    in0=back_tiles[k][:].rearrange("p (j m) -> p m j", j=BLOCKS)[:, cols, :],
                    in1=decay_tiles[k][:].rearrange("p (m j) -> p m j", j=BLOCKS)[:, cols, :],
                    op=ALU.add,
                )
                nc.sync.dma_start(out=rows_of(out, c)[:, i, ncols], in_=result[:, ncols])

        def turn(k):
            for bank in range(ROW_TILES[k // STEPS] // 2):
                turn_half(k, bank)
                group_half(k, bank)

        def live(k):
            return 0 <= k < UNITS

        def permute(k):
            if k < 2:
                permute_scales(k)
                permute_words(2 * k)
                permute_words(2 * k + 1)

        def load(k):
            c, q = divmod(k, STEPS)
            if q == 0 and 0 < c < N_CHUNKS - 1:
                load_spk(c + 1)
                load_b(c + 1)
                load_x(c + 1)
                load_mem(c + 1)

        step = ((load, 4), (quantise, 3), (permute, 2), (update, -1), (decay, 0), (finish, -6), (threshold, 2), (reset, 2), (decay_rest, -1), (matmuls, 0), (offset, 0), (spike_part, 3), (early_matmuls, 1), (turn, 5), (turn_back, -5), (turn_b, 4), (spread, 7))
        constants()
        for n in range(-TURN_LEAD, UNITS + FINISH_LAG):
            for stage, offset_in_units in step:
                if live(n + offset_in_units):
                    stage(n + offset_in_units)
            if n == -TURN_LEAD + 2:
                decay_rows()
                bias_constants()
